import numpy as np
import ml_dtypes

BF16 = ml_dtypes.bfloat16


def bf(x):
    return np.asarray(x, np.float32).astype(BF16)


def f32(x):
    return np.asarray(x, np.float32)


def f64(x):
    return np.asarray(x).astype(np.float64)


def striped(idx):
    return np.tile(idx.reshape(-1, 16).T, (8, 1))


C, S, N, W = 1024, 256, 128, 2


def setup_inputs():
    return {"x": bf(np.random.standard_normal((C, N))), "wq": bf(np.random.standard_normal((C, C)) / np.sqrt(C)), "bq": f32(0.1 * np.random.standard_normal((C, 1))), "wv": bf(np.random.standard_normal((C, C)) / np.sqrt(C)), "bv": f32(0.1 * np.random.standard_normal((C, 1))), "base": f32(np.random.standard_normal((C, S))), "offs": striped(np.random.permutation(S)[:N])}


def reference(x, wq, bq, wv, bv, base, offs):
    idx = offs[:16].T.reshape(-1)
    xs = f64(x)
    q = f64(wq).T @ xs + f64(bq)
    v = f64(wv).T @ xs + f64(bv)
    num = np.zeros_like(q)
    den = np.zeros_like(q)
    for t in range(-W, W + 1):
        e = np.exp(q * np.roll(xs, -t, axis=1))
        num = num + e * np.roll(v, -t, axis=1)
        den = den + e
    res = f64(base).copy()
    res[:, idx] = num * (1.0 / den)
    return res

@@ -1,0 +1,105 @@
+import concourse.mybir as mybir
+from concourse.masks import make_identity
+
+F32 = mybir.dt.float32
+BF16 = mybir.dt.bfloat16
+U16 = mybir.dt.uint16
+ADD = mybir.AluOpType.add
+MULT = mybir.AluOpType.mult
+EXP = mybir.ActivationFunctionType.Exp
+
+P = 128
+C = 1024
+N = 128
+S = 256
+W = 2
+T = 2 * W + 1
+NB = C // P
+GC = 256
+BPG = GC // P
+X0 = 16
+XROW = 160
+
+FLOPS = 2 * 2 * C * C * N
+
+
+def tile_slidingwindowattention_s_kernel(tc, x, wq, bq, wv, bv, base, offs, out):
+    nc = tc.nc
+    x_blocks = x.rearrange("(b p) j -> p b j", p=P)
+    wq_blocks = wq.rearrange("(k p) c -> p k c", p=P)
+    wv_blocks = wv.rearrange("(k p) c -> p k c", p=P)
+
+    with (
+        tc.tile_pool(name="held", bufs=1) as held,
+        tc.tile_pool(name="work", bufs=2) as work,
+        tc.psum_pool(name="psum", bufs=3) as psum,
+        tc.psum_pool(name="psum_once", bufs=1) as psum_once,
+    ):
+        offsets = held.tile([P, N // 16], U16, name="offsets")
+        nc.sync.dma_start(offsets[:], offs)
+
+        xpad = held.tile([P, NB, XROW], BF16, name="xpad")
+        nc.sync.dma_start(xpad[:, :, X0 : X0 + N], x_blocks)
+        nc.vector.tensor_copy(xpad[:, :, X0 - W : X0], xpad[:, :, X0 + N - W : X0 + N])
+        nc.vector.tensor_copy(xpad[:, :, X0 + N : X0 + N + W], xpad[:, :, X0 : X0 + W])
+
+        bias_rows = held.tile([2 * NB, P], F32, name="bias_rows")
+        nc.sync.dma_start(bias_rows[0:NB, :], bq.rearrange("(b p) o -> b (p o)", p=P))
+        nc.sync.dma_start(bias_rows[NB : 2 * NB, :], bv.rearrange("(b p) o -> b (p o)", p=P))
+        ident = held.tile([2 * NB, 2 * NB], F32, name="ident")
+        make_identity(nc, ident[:])
+        bias_ps = psum_once.tile([P, 2 * NB], F32, name="bias_ps")
+        nc.tensor.matmul(bias_ps[:], lhsT=bias_rows[:], rhs=ident[:], start=True, stop=True)
+        bias = held.tile([P, 2 * NB], F32, name="bias")
+        nc.vector.tensor_copy(bias[:], bias_ps[:])
+
+        wq_sb, wv_sb, windows = [], [], []
+        for g in range(NB // BPG):
+            wq_g = held.tile([P, NB, GC], BF16, name=f"wq{g}")
+            nc.sync.dma_start(wq_g[:], wq_blocks[:, :, g * GC : (g + 1) * GC])
+            wq_sb.append(wq_g)
+            wv_g = held.tile([P, NB, GC], BF16, name=f"wv{g}")
+            nc.sync.dma_start(wv_g[:], wv_blocks[:, :, g * GC : (g + 1) * GC])
+            wv_sb.append(wv_g)
+            for b in range(g * BPG, (g + 1) * BPG):
+                window = held.tile([P, S], F32, name=f"window{b}")
+                nc.sync.dma_start(window[:], base[b * P : (b + 1) * P, :])
+                windows.append(window)
+
+        for b in range(NB):
+            g, cols = b // BPG, slice((b % BPG) * P, (b % BPG + 1) * P)
+
+            q_ps = psum.tile([P, N], F32, name="q_ps")
+            for k in range(NB):
+                nc.tensor.matmul(q_ps[:], lhsT=wq_sb[g][:, k, cols], rhs=xpad[:, k, X0 : X0 + N],
+                                 start=(k == 0), stop=(k == NB - 1))
+            v_ps = psum.tile([P, N + 2 * W], F32, name="v_ps")
+            for k in range(NB):
+                nc.tensor.matmul(v_ps[:], lhsT=wv_sb[g][:, k, cols], rhs=xpad[:, k, X0 - W : X0 + N + W],
+                                 start=(k == 0), stop=(k == NB - 1))
+
+            scores = work.tile([P, T, N], F32, name="scores")
+            for t in range(T):
+                nc.vector.scalar_tensor_tensor(
+                    out=scores[:, t, :], in0=q_ps[:], scalar=bias[:, b : b + 1],
+                    in1=xpad[:, b, X0 - W + t : X0 - W + t + N], op0=ADD, op1=MULT)
+
+            terms = work.tile([P, 2, T, N], F32, name="terms")
+            nc.scalar.activation(terms[:, 0, :, :], scores[:], EXP)
+            for t in range(T):
+                nc.vector.scalar_tensor_tensor(
+                    out=terms[:, 1, t, :], in0=v_ps[:, t : t + N], scalar=bias[:, NB + b : NB + b + 1],
+                    in1=terms[:, 0, t, :], op0=ADD, op1=MULT)
+
+            pairs = work.tile([P, 2, 2, N], F32, name="pairs")
+            nc.vector.tensor_tensor(pairs[:], terms[:, :, 0:2, :], terms[:, :, 2:4, :], ADD)
+            four = work.tile([P, 2, N], F32, name="four")
+            nc.vector.tensor_tensor(four[:], pairs[:, :, 0, :], pairs[:, :, 1, :], ADD)
+            sums = work.tile([P, 2, N], F32, name="sums")
+            nc.vector.tensor_tensor(sums[:], four[:], terms[:, :, 4, :], ADD)
+
+            rden = work.tile([P, N], F32, name="rden")
+            nc.vector.reciprocal(rden[:], sums[:, 0, :])
+
+            nc.vector.tensor_tensor(windows[b][:].indirect(offsets[:]), sums[:, 1, :], rden[:], MULT)
+            nc.sync.dma_start(out[b * P : (b + 1) * P, :], windows[b][:])

@@ -31,7 +31,7 @@ def tile_slidingwindowattention_s_kernel(tc, x, wq, bq, wv, bv, base, offs, out)
 
     with (
         tc.tile_pool(name="held", bufs=1) as held,
-        tc.tile_pool(name="work", bufs=2) as work,
+        tc.tile_pool(name="work", bufs=3) as work,
         tc.psum_pool(name="psum", bufs=3) as psum,
         tc.psum_pool(name="psum_once", bufs=1) as psum_once,
     ):
@@ -92,11 +92,11 @@ def tile_slidingwindowattention_s_kernel(tc, x, wq, bq, wv, bv, base, offs, out)
                     in1=terms[:, 0, t, :], op0=ADD, op1=MULT)
 
             pairs = work.tile([P, 2, 2, N], F32, name="pairs")
-            nc.vector.tensor_tensor(pairs[:], terms[:, :, 0:2, :], terms[:, :, 2:4, :], ADD)
+            nc.gpsimd.tensor_tensor(pairs[:], terms[:, :, 0:2, :], terms[:, :, 2:4, :], ADD)
             four = work.tile([P, 2, N], F32, name="four")
-            nc.vector.tensor_tensor(four[:], pairs[:, :, 0, :], pairs[:, :, 1, :], ADD)
+            nc.gpsimd.tensor_tensor(four[:], pairs[:, :, 0, :], pairs[:, :, 1, :], ADD)
             sums = work.tile([P, 2, N], F32, name="sums")
-            nc.vector.tensor_tensor(sums[:], four[:], terms[:, :, 4, :], ADD)
+            nc.gpsimd.tensor_tensor(sums[:], four[:], terms[:, :, 4, :], ADD)
 
             rden = work.tile([P, N], F32, name="rden")
             nc.vector.reciprocal(rden[:], sums[:, 0, :])

@@ -31,75 +31,99 @@ def tile_slidingwindowattention_s_kernel(tc, x, wq, bq, wv, bv, base, offs, out)
 
     with (
         tc.tile_pool(name="held", bufs=1) as held,
-        tc.tile_pool(name="work", bufs=3) as work,
-        tc.psum_pool(name="psum", bufs=3) as psum,
-        tc.psum_pool(name="psum_once", bufs=1) as psum_once,
+        tc.tile_pool(name="work", bufs=4) as work,
+        tc.psum_pool(name="psum_q", bufs=2) as psum_q,
+        tc.psum_pool(name="psum_v", bufs=3) as psum_v,
+        tc.psum_pool(name="psum_flipped", bufs=2) as psum_flipped,
+        tc.psum_pool(name="psum_back", bufs=1) as psum_back,
     ):
-        offsets = held.tile([P, N // 16], U16, name="offsets")
-        nc.sync.dma_start(offsets[:], offs)
-
         xpad = held.tile([P, NB, XROW], BF16, name="xpad")
         nc.sync.dma_start(xpad[:, :, X0 : X0 + N], x_blocks)
         nc.vector.tensor_copy(xpad[:, :, X0 - W : X0], xpad[:, :, X0 + N - W : X0 + N])
         nc.vector.tensor_copy(xpad[:, :, X0 + N : X0 + N + W], xpad[:, :, X0 : X0 + W])
 
-        bias_rows = held.tile([2 * NB, P], F32, name="bias_rows")
-        nc.sync.dma_start(bias_rows[0:NB, :], bq.rearrange("(b p) o -> b (p o)", p=P))
-        nc.sync.dma_start(bias_rows[NB : 2 * NB, :], bv.rearrange("(b p) o -> b (p o)", p=P))
-        ident = held.tile([2 * NB, 2 * NB], F32, name="ident")
+        ident = held.tile([P, P], F32, name="ident")
         make_identity(nc, ident[:])
-        bias_ps = psum_once.tile([P, 2 * NB], F32, name="bias_ps")
-        nc.tensor.matmul(bias_ps[:], lhsT=bias_rows[:], rhs=ident[:], start=True, stop=True)
-        bias = held.tile([P, 2 * NB], F32, name="bias")
-        nc.vector.tensor_copy(bias[:], bias_ps[:])
 
+        bias = held.tile([P, 2 * NB], F32, name="bias")
         wq_sb, wv_sb, windows = [], [], []
         for g in range(NB // BPG):
             wq_g = held.tile([P, NB, GC], BF16, name=f"wq{g}")
             nc.sync.dma_start(wq_g[:], wq_blocks[:, :, g * GC : (g + 1) * GC])
             wq_sb.append(wq_g)
             wv_g = held.tile([P, NB, GC], BF16, name=f"wv{g}")
-            nc.sync.dma_start(wv_g[:], wv_blocks[:, :, g * GC : (g + 1) * GC])
+            nc.scalar.dma_start(wv_g[:], wv_blocks[:, :, g * GC : (g + 1) * GC])
             wv_sb.append(wv_g)
-            for b in range(g * BPG, (g + 1) * BPG):
-                window = held.tile([P, S], F32, name=f"window{b}")
-                nc.sync.dma_start(window[:], base[b * P : (b + 1) * P, :])
-                windows.append(window)
-
+            if g == 0:
+                with nc.allow_non_contiguous_dma(reason="two small vectors, one element to a partition and block"):
+                    nc.sync.dma_start(bias[:, 0:NB], bq.rearrange("(b p) o -> p (b o)", p=P))
+                    nc.sync.dma_start(bias[:, NB : 2 * NB], bv.rearrange("(b p) o -> p (b o)", p=P))
+        offsets = held.tile([P, N // 16], U16, name="offsets")
+        nc.sync.dma_start(offsets[:], offs)
         for b in range(NB):
-            g, cols = b // BPG, slice((b % BPG) * P, (b % BPG + 1) * P)
+            window = held.tile([P, S], F32, name=f"window{b}")
+            nc.sync.dma_start(window[:], base[b * P : (b + 1) * P, :])
+            windows.append(window)
 
-            q_ps = psum.tile([P, N], F32, name="q_ps")
+        v_of, e_of, num_of, rden_of = {}, {}, {}, {}
+
+        def score(b):
+            g, cols = b // BPG, slice((b % BPG) * P, (b % BPG + 1) * P)
+            q_ps = psum_q.tile([P, N], F32, name="q_ps")
             for k in range(NB):
                 nc.tensor.matmul(q_ps[:], lhsT=wq_sb[g][:, k, cols], rhs=xpad[:, k, X0 : X0 + N],
                                  start=(k == 0), stop=(k == NB - 1))
-            v_ps = psum.tile([P, N + 2 * W], F32, name="v_ps")
+            v_ps = psum_v.tile([P, N + 2 * W], F32, name="v_ps")
             for k in range(NB):
                 nc.tensor.matmul(v_ps[:], lhsT=wv_sb[g][:, k, cols], rhs=xpad[:, k, X0 - W : X0 + N + W],
                                  start=(k == 0), stop=(k == NB - 1))
-
             scores = work.tile([P, T, N], F32, name="scores")
             for t in range(T):
                 nc.vector.scalar_tensor_tensor(
                     out=scores[:, t, :], in0=q_ps[:], scalar=bias[:, b : b + 1],
                     in1=xpad[:, b, X0 - W + t : X0 - W + t + N], op0=ADD, op1=MULT)
+            e = work.tile([P, T, N], F32, name="e")
+            nc.scalar.activation(e[:], scores[:], EXP)
+            v_of[b], e_of[b] = v_ps, e
 
-            terms = work.tile([P, 2, T, N], F32, name="terms")
-            nc.scalar.activation(terms[:, 0, :, :], scores[:], EXP)
+        def weigh(b):
+            v_ps, e = v_of[b], e_of[b]
+            weighed = work.tile([P, T, N], F32, name="weighed")
             for t in range(T):
                 nc.vector.scalar_tensor_tensor(
-                    out=terms[:, 1, t, :], in0=v_ps[:, t : t + N], scalar=bias[:, NB + b : NB + b + 1],
-                    in1=terms[:, 0, t, :], op0=ADD, op1=MULT)
+                    out=weighed[:, t, :], in0=v_ps[:, t : t + N], scalar=bias[:, NB + b : NB + b + 1],
+                    in1=e[:, t, :], op0=ADD, op1=MULT)
+            pairs = work.tile([P, 2, N], F32, name="pairs")
+            nc.gpsimd.tensor_tensor(pairs[:], weighed[:, 0:2, :], weighed[:, 2:4, :], ADD)
+            four = work.tile([P, N], F32, name="four")
+            nc.gpsimd.tensor_tensor(four[:], pairs[:, 0, :], pairs[:, 1, :], ADD)
+            num = work.tile([P, N], F32, name="num")
+            nc.gpsimd.tensor_tensor(num[:], four[:], weighed[:, 4, :], ADD)
+            num_of[b] = num
 
-            pairs = work.tile([P, 2, 2, N], F32, name="pairs")
-            nc.gpsimd.tensor_tensor(pairs[:], terms[:, :, 0:2, :], terms[:, :, 2:4, :], ADD)
-            four = work.tile([P, 2, N], F32, name="four")
-            nc.gpsimd.tensor_tensor(four[:], pairs[:, :, 0, :], pairs[:, :, 1, :], ADD)
-            sums = work.tile([P, 2, N], F32, name="sums")
-            nc.gpsimd.tensor_tensor(sums[:], four[:], terms[:, :, 4, :], ADD)
-
+        def invert(b):
+            e = e_of[b]
+            den_flipped = psum_flipped.tile([P, P], F32, name="den_flipped")
+            for t in range(T):
+                nc.tensor.matmul(den_flipped[:], lhsT=e[:, t, :], rhs=ident[:],
+                                 is_transpose=True, start=(t == 0), stop=(t == T - 1))
+            rden_flipped = work.tile([P, P], F32, name="rden_flipped")
+            nc.vector.reciprocal(rden_flipped[:], den_flipped[:])
+            rden_ps = psum_back.tile([P, N], F32, name="rden_ps")
+            nc.tensor.transpose(rden_ps[:], rden_flipped[:], ident[:])
             rden = work.tile([P, N], F32, name="rden")
-            nc.vector.reciprocal(rden[:], sums[:, 0, :])
+            nc.scalar.copy(rden[:], rden_ps[:])
+            rden_of[b] = rden
 
-            nc.vector.tensor_tensor(windows[b][:].indirect(offsets[:]), sums[:, 1, :], rden[:], MULT)
+        def place(b):
+            nc.vector.tensor_tensor(windows[b][:].indirect(offsets[:]), num_of[b][:], rden_of[b][:], MULT)
             nc.sync.dma_start(out[b * P : (b + 1) * P, :], windows[b][:])
+
+        for i in range(NB + 2):
+            if i < NB:
+                score(i)
+            if 0 <= i - 1 < NB:
+                weigh(i - 1)
+                invert(i - 1)
+            if 0 <= i - 2 < NB:
+                place(i - 2)

@@ -19,6 +19,8 @@ GC = 256
 BPG = GC // P
 X0 = 16
 XROW = 160
+WARM_COLS = 512
+WARM_MATMULS = 4
 
 FLOPS = 2 * 2 * C * C * N
 
@@ -39,31 +41,41 @@ def tile_slidingwindowattention_s_kernel(tc, x, wq, bq, wv, bv, base, offs, out)
     ):
         xpad = held.tile([P, NB, XROW], BF16, name="xpad")
         nc.sync.dma_start(xpad[:, :, X0 : X0 + N], x_blocks)
-        nc.vector.tensor_copy(xpad[:, :, X0 - W : X0], xpad[:, :, X0 + N - W : X0 + N])
-        nc.vector.tensor_copy(xpad[:, :, X0 + N : X0 + N + W], xpad[:, :, X0 : X0 + W])
-
-        ident = held.tile([P, P], F32, name="ident")
-        make_identity(nc, ident[:])
-
-        bias = held.tile([P, 2 * NB], F32, name="bias")
+        bias_rows = held.tile([2 * NB, P], F32, name="bias_rows")
+        offsets = held.tile([P, N // 16], U16, name="offsets")
         wq_sb, wv_sb, windows = [], [], []
         for g in range(NB // BPG):
             wq_g = held.tile([P, NB, GC], BF16, name=f"wq{g}")
             nc.sync.dma_start(wq_g[:], wq_blocks[:, :, g * GC : (g + 1) * GC])
             wq_sb.append(wq_g)
+            if g == 0:
+                nc.sync.dma_start(bias_rows[0:NB, :], bq.rearrange("(b p) o -> b (p o)", p=P))
+                nc.sync.dma_start(bias_rows[NB : 2 * NB, :], bv.rearrange("(b p) o -> b (p o)", p=P))
             wv_g = held.tile([P, NB, GC], BF16, name=f"wv{g}")
-            nc.scalar.dma_start(wv_g[:], wv_blocks[:, :, g * GC : (g + 1) * GC])
+            nc.sync.dma_start(wv_g[:], wv_blocks[:, :, g * GC : (g + 1) * GC])
             wv_sb.append(wv_g)
             if g == 0:
-                with nc.allow_non_contiguous_dma(reason="two small vectors, one element to a partition and block"):
-                    nc.sync.dma_start(bias[:, 0:NB], bq.rearrange("(b p) o -> p (b o)", p=P))
-                    nc.sync.dma_start(bias[:, NB : 2 * NB], bv.rearrange("(b p) o -> p (b o)", p=P))
-        offsets = held.tile([P, N // 16], U16, name="offsets")
-        nc.sync.dma_start(offsets[:], offs)
-        for b in range(NB):
-            window = held.tile([P, S], F32, name=f"window{b}")
-            nc.sync.dma_start(window[:], base[b * P : (b + 1) * P, :])
-            windows.append(window)
+                nc.sync.dma_start(offsets[:], offs)
+            for b in range(g * BPG, (g + 1) * BPG):
+                window = held.tile([P, S], F32, name=f"window{b}")
+                nc.sync.dma_start(window[:], base[b * P : (b + 1) * P, :])
+                windows.append(window)
+
+        zeros = held.tile([P, WARM_COLS], BF16, name="zeros")
+        nc.vector.memset(zeros[:], 0.0)
+        warm_ps = psum_back.tile([P, WARM_COLS], F32, name="warm_ps", tag="rden_ps")
+        for i in range(WARM_MATMULS):
+            nc.tensor.matmul(warm_ps[:], lhsT=zeros[:, 0:P], rhs=zeros[:], start=True, stop=True)
+
+        nc.vector.tensor_copy(xpad[:, :, X0 - W : X0], xpad[:, :, X0 + N - W : X0 + N])
+        nc.vector.tensor_copy(xpad[:, :, X0 + N : X0 + N + W], xpad[:, :, X0 : X0 + W])
+
+        ident = held.tile([P, P], F32, name="ident")
+        make_identity(nc, ident[:])
+        bias_ps = psum_back.tile([P, 2 * NB], F32, name="bias_ps", tag="rden_ps")
+        nc.tensor.matmul(bias_ps[:], lhsT=bias_rows[:], rhs=ident[0 : 2 * NB, 0 : 2 * NB], start=True, stop=True)
+        bias = held.tile([P, 2 * NB], F32, name="bias")
+        nc.vector.tensor_copy(bias[:], bias_ps[:])
 
         v_of, e_of, num_of, rden_of = {}, {}, {}, {}
 
@@ -119,11 +131,11 @@ def tile_slidingwindowattention_s_kernel(tc, x, wq, bq, wv, bv, base, offs, out)
             nc.vector.tensor_tensor(windows[b][:].indirect(offsets[:]), num_of[b][:], rden_of[b][:], MULT)
             nc.sync.dma_start(out[b * P : (b + 1) * P, :], windows[b][:])
 
-        for i in range(NB + 2):
+        for i in range(NB + 3):
             if i < NB:
                 score(i)
             if 0 <= i - 1 < NB:
                 weigh(i - 1)
                 invert(i - 1)
-            if 0 <= i - 2 < NB:
-                place(i - 2)
+            if 0 <= i - 3 < NB:
+                place(i - 3)

@@ -7,6 +7,8 @@ U16 = mybir.dt.uint16
 ADD = mybir.AluOpType.add
 MULT = mybir.AluOpType.mult
 EXP = mybir.ActivationFunctionType.Exp
+ABS_RSQRT = mybir.ActivationFunctionType.Abs_reciprocal_sqrt
+SQUARE = mybir.ActivationFunctionType.Square
 
 P = 128
 C = 1024
@@ -17,6 +19,7 @@ T = 2 * W + 1
 NB = C // P
 GC = 256
 BPG = GC // P
+HALF = NB // 2
 X0 = 16
 XROW = 160
 WARM_COLS = 512
@@ -34,6 +37,7 @@ def tile_slidingwindowattention_s_kernel(tc, x, wq, bq, wv, bv, base, offs, out)
     with (
         tc.tile_pool(name="held", bufs=1) as held,
         tc.tile_pool(name="work", bufs=4) as work,
+        tc.tile_pool(name="kept", bufs=6) as kept,
         tc.psum_pool(name="psum_q", bufs=2) as psum_q,
         tc.psum_pool(name="psum_v", bufs=3) as psum_v,
         tc.psum_pool(name="psum_flipped", bufs=2) as psum_flipped,
@@ -54,16 +58,15 @@ def tile_slidingwindowattention_s_kernel(tc, x, wq, bq, wv, bv, base, offs, out)
             wv_g = held.tile([P, NB, GC], BF16, name=f"wv{g}")
             nc.sync.dma_start(wv_g[:], wv_blocks[:, :, g * GC : (g + 1) * GC])
             wv_sb.append(wv_g)
-            if g == 0:
-                nc.sync.dma_start(offsets[:], offs)
-            for b in range(g * BPG, (g + 1) * BPG):
-                window = held.tile([P, S], F32, name=f"window{b}")
-                nc.sync.dma_start(window[:], base[b * P : (b + 1) * P, :])
-                windows.append(window)
+        nc.sync.dma_start(offsets[:], offs)
+        for b in range(NB):
+            window = held.tile([P, S], F32, name=f"window{b}")
+            nc.sync.dma_start(window[:], base[b * P : (b + 1) * P, :])
+            windows.append(window)
 
         zeros = held.tile([P, WARM_COLS], BF16, name="zeros")
         nc.vector.memset(zeros[:], 0.0)
-        warm_ps = psum_back.tile([P, WARM_COLS], F32, name="warm_ps", tag="rden_ps")
+        warm_ps = psum_back.tile([P, WARM_COLS], F32, name="warm_ps", tag="back_ps")
         for i in range(WARM_MATMULS):
             nc.tensor.matmul(warm_ps[:], lhsT=zeros[:, 0:P], rhs=zeros[:], start=True, stop=True)
 
@@ -72,12 +75,12 @@ def tile_slidingwindowattention_s_kernel(tc, x, wq, bq, wv, bv, base, offs, out)
 
         ident = held.tile([P, P], F32, name="ident")
         make_identity(nc, ident[:])
-        bias_ps = psum_back.tile([P, 2 * NB], F32, name="bias_ps", tag="rden_ps")
+        bias_ps = psum_back.tile([P, 2 * NB], F32, name="bias_ps", tag="back_ps")
         nc.tensor.matmul(bias_ps[:], lhsT=bias_rows[:], rhs=ident[0 : 2 * NB, 0 : 2 * NB], start=True, stop=True)
         bias = held.tile([P, 2 * NB], F32, name="bias")
         nc.vector.tensor_copy(bias[:], bias_ps[:])
 
-        v_of, e_of, num_of, rden_of = {}, {}, {}, {}
+        v_of, e_of, num_of, den_flipped_of, rden_of = {}, {}, {}, {}, {}
 
         def score(b):
             g, cols = b // BPG, slice((b % BPG) * P, (b % BPG + 1) * P)
@@ -109,33 +112,38 @@ def tile_slidingwindowattention_s_kernel(tc, x, wq, bq, wv, bv, base, offs, out)
             nc.gpsimd.tensor_tensor(pairs[:], weighed[:, 0:2, :], weighed[:, 2:4, :], ADD)
             four = work.tile([P, N], F32, name="four")
             nc.gpsimd.tensor_tensor(four[:], pairs[:, 0, :], pairs[:, 1, :], ADD)
-            num = work.tile([P, N], F32, name="num")
+            num = kept.tile([P, N], F32, name="num")
             nc.gpsimd.tensor_tensor(num[:], four[:], weighed[:, 4, :], ADD)
             num_of[b] = num
 
-        def invert(b):
-            e = e_of[b]
-            den_flipped = psum_flipped.tile([P, P], F32, name="den_flipped")
+        def add_den(b):
+            if b % HALF == 0:
+                den_flipped_of[b // HALF] = psum_flipped.tile([P, HALF, P], F32, name="den_flipped")
             for t in range(T):
-                nc.tensor.matmul(den_flipped[:], lhsT=e[:, t, :], rhs=ident[:],
+                nc.tensor.matmul(den_flipped_of[b // HALF][:, b % HALF, :], lhsT=e_of[b][:, t, :], rhs=ident[:],
                                  is_transpose=True, start=(t == 0), stop=(t == T - 1))
-            rden_flipped = work.tile([P, P], F32, name="rden_flipped")
-            nc.vector.reciprocal(rden_flipped[:], den_flipped[:])
-            rden_ps = psum_back.tile([P, N], F32, name="rden_ps")
-            nc.tensor.transpose(rden_ps[:], rden_flipped[:], ident[:])
-            rden = work.tile([P, N], F32, name="rden")
-            nc.scalar.copy(rden[:], rden_ps[:])
-            rden_of[b] = rden
+
+        def invert(h):
+            root_flipped = work.tile([P, HALF, P], F32, name="root_flipped")
+            nc.scalar.activation(root_flipped[:], den_flipped_of[h][:], ABS_RSQRT)
+            for i in range(HALF):
+                back_ps = psum_back.tile([P, N], F32, name="back_ps")
+                nc.tensor.transpose(back_ps[:], root_flipped[:, i, :], ident[:])
+                rden = kept.tile([P, N], F32, name="rden")
+                nc.scalar.activation(rden[:], back_ps[:], SQUARE)
+                rden_of[h * HALF + i] = rden
 
         def place(b):
             nc.vector.tensor_tensor(windows[b][:].indirect(offsets[:]), num_of[b][:], rden_of[b][:], MULT)
             nc.sync.dma_start(out[b * P : (b + 1) * P, :], windows[b][:])
 
-        for i in range(NB + 3):
+        for i in range(NB + 5):
             if i < NB:
                 score(i)
             if 0 <= i - 1 < NB:
                 weigh(i - 1)
-                invert(i - 1)
-            if 0 <= i - 3 < NB:
-                place(i - 3)
+                add_den(i - 1)
+                if i % HALF == 0:
+                    invert((i - 1) // HALF)
+            if 0 <= i - 5 < NB:
+                place(i - 5)

@@ -22,6 +22,9 @@ BPG = GC // P
 HALF = NB // 2
 X0 = 16
 XROW = 160
+VROW = N + 2 * W
+EROW = VROW + 1
+E_BUFS = 4
 WARM_COLS = 512
 WARM_MATMULS = 4
 
@@ -80,6 +83,12 @@ def tile_slidingwindowattention_s_kernel(tc, x, wq, bq, wv, bv, base, offs, out)
         bias = held.tile([P, 2 * NB], F32, name="bias")
         nc.vector.tensor_copy(bias[:], bias_ps[:])
 
+        e_tiles = []
+        for i in range(E_BUFS):
+            e_tile = held.tile([P, T * EROW], F32, name=f"e{i}")
+            nc.gpsimd.memset(e_tile[:], 0.0)
+            e_tiles.append(e_tile)
+
         v_of, e_of, num_of, den_flipped_of, rden_of = {}, {}, {}, {}, {}
 
         def score(b):
@@ -97,17 +106,19 @@ def tile_slidingwindowattention_s_kernel(tc, x, wq, bq, wv, bv, base, offs, out)
                 nc.vector.scalar_tensor_tensor(
                     out=scores[:, t, :], in0=q_ps[:], scalar=bias[:, b : b + 1],
                     in1=xpad[:, b, X0 - W + t : X0 - W + t + N], op0=ADD, op1=MULT)
-            e = work.tile([P, T, N], F32, name="e")
-            nc.scalar.activation(e[:], scores[:], EXP)
-            v_of[b], e_of[b] = v_ps, e
+            e_tile = e_tiles[b % E_BUFS]
+            e = e_tile[:].rearrange("p (t r) -> p t r", r=EROW)[:, :, 0:N]
+            nc.scalar.activation(e, scores[:], EXP)
+            v_of[b], e_of[b] = v_ps, e_tile
 
         def weigh(b):
-            v_ps, e = v_of[b], e_of[b]
-            weighed = work.tile([P, T, N], F32, name="weighed")
-            for t in range(T):
-                nc.vector.scalar_tensor_tensor(
-                    out=weighed[:, t, :], in0=v_ps[:, t : t + N], scalar=bias[:, NB + b : NB + b + 1],
-                    in1=e[:, t, :], op0=ADD, op1=MULT)
+            v_ps, e_tile = v_of[b], e_of[b]
+            weighed_tile = work.tile([P, T * EROW], F32, name="weighed_tile")
+            nc.vector.scalar_tensor_tensor(
+                out=weighed_tile[:, 0 : T * VROW].rearrange("p (t i) -> p t i", i=VROW),
+                in0=v_ps[:].unsqueeze(1).to_broadcast([P, T, VROW]), scalar=bias[:, NB + b : NB + b + 1],
+                in1=e_tile[:, 0 : T * VROW].rearrange("p (t i) -> p t i", i=VROW), op0=ADD, op1=MULT)
+            weighed = weighed_tile[:].rearrange("p (t r) -> p t r", r=EROW)[:, :, 0:N]
             pairs = work.tile([P, 2, N], F32, name="pairs")
             nc.gpsimd.tensor_tensor(pairs[:], weighed[:, 0:2, :], weighed[:, 2:4, :], ADD)
             four = work.tile([P, N], F32, name="four")
@@ -120,7 +131,8 @@ def tile_slidingwindowattention_s_kernel(tc, x, wq, bq, wv, bv, base, offs, out)
             if b % HALF == 0:
                 den_flipped_of[b // HALF] = psum_flipped.tile([P, HALF, P], F32, name="den_flipped")
             for t in range(T):
-                nc.tensor.matmul(den_flipped_of[b // HALF][:, b % HALF, :], lhsT=e_of[b][:, t, :], rhs=ident[:],
+                nc.tensor.matmul(den_flipped_of[b // HALF][:, b % HALF, :],
+                                 lhsT=e_of[b][:, t * EROW : t * EROW + N], rhs=ident[:],
                                  is_transpose=True, start=(t == 0), stop=(t == T - 1))
 
         def invert(h):

@@ -25,6 +25,7 @@ XROW = 160
 VROW = N + 2 * W
 EROW = VROW + 1
 E_BUFS = 4
+XREP = 672
 WARM_COLS = 512
 WARM_MATMULS = 4
 
@@ -75,6 +76,9 @@ def tile_slidingwindowattention_s_kernel(tc, x, wq, bq, wv, bv, base, offs, out)
 
         nc.vector.tensor_copy(xpad[:, :, X0 - W : X0], xpad[:, :, X0 + N - W : X0 + N])
         nc.vector.tensor_copy(xpad[:, :, X0 + N : X0 + N + W], xpad[:, :, X0 : X0 + W])
+        xrep = held.tile([P, NB, XREP], BF16, name="xrep")
+        for t in range(T):
+            nc.vector.tensor_copy(xrep[:, :, t * VROW : (t + 1) * VROW], xpad[:, :, X0 - W : X0 + N + W])
 
         ident = held.tile([P, P], F32, name="ident")
         make_identity(nc, ident[:])
@@ -86,7 +90,7 @@ def tile_slidingwindowattention_s_kernel(tc, x, wq, bq, wv, bv, base, offs, out)
         e_tiles = []
         for i in range(E_BUFS):
             e_tile = held.tile([P, T * EROW], F32, name=f"e{i}")
-            nc.gpsimd.memset(e_tile[:], 0.0)
+            nc.vector.memset(e_tile[:].rearrange("p (t r) -> p t r", r=EROW)[:, :, N:EROW], 0.0)
             e_tiles.append(e_tile)
 
         v_of, e_of, num_of, den_flipped_of, rden_of = {}, {}, {}, {}, {}
@@ -102,10 +106,9 @@ def tile_slidingwindowattention_s_kernel(tc, x, wq, bq, wv, bv, base, offs, out)
                 nc.tensor.matmul(v_ps[:], lhsT=wv_sb[g][:, k, cols], rhs=xpad[:, k, X0 - W : X0 + N + W],
                                  start=(k == 0), stop=(k == NB - 1))
             scores = work.tile([P, T, N], F32, name="scores")
-            for t in range(T):
-                nc.vector.scalar_tensor_tensor(
-                    out=scores[:, t, :], in0=q_ps[:], scalar=bias[:, b : b + 1],
-                    in1=xpad[:, b, X0 - W + t : X0 - W + t + N], op0=ADD, op1=MULT)
+            nc.vector.scalar_tensor_tensor(
+                out=scores[:], in0=q_ps[:].unsqueeze(1).to_broadcast([P, T, N]), scalar=bias[:, b : b + 1],
+                in1=xrep[:, b, 0 : T * EROW].rearrange("p (t r) -> p t r", r=EROW)[:, :, 0:N], op0=ADD, op1=MULT)
             e_tile = e_tiles[b % E_BUFS]
             e = e_tile[:].rearrange("p (t r) -> p t r", r=EROW)[:, :, 0:N]
             nc.scalar.activation(e, scores[:], EXP)

@@ -19,7 +19,9 @@ T = 2 * W + 1
 NB = C // P
 GC = 256
 BPG = GC // P
-HALF = NB // 2
+DEN_TILES = ((0, 1, 2, 3), (4, 5, 6, 7))
+INVERT_AFTER = (3, 7)
+VECTOR_ADDS = 2
 X0 = 16
 XROW = 160
 VROW = N + 2 * W
@@ -41,15 +43,14 @@ def tile_slidingwindowattention_s_kernel(tc, x, wq, bq, wv, bv, base, offs, out)
     with (
         tc.tile_pool(name="held", bufs=1) as held,
         tc.tile_pool(name="work", bufs=4) as work,
-        tc.tile_pool(name="kept", bufs=6) as kept,
         tc.psum_pool(name="psum_q", bufs=2) as psum_q,
-        tc.psum_pool(name="psum_v", bufs=3) as psum_v,
+        tc.psum_pool(name="psum_v", bufs=2) as psum_v,
         tc.psum_pool(name="psum_flipped", bufs=2) as psum_flipped,
-        tc.psum_pool(name="psum_back", bufs=1) as psum_back,
+        tc.psum_pool(name="psum_back", bufs=2) as psum_back,
     ):
         xpad = held.tile([P, NB, XROW], BF16, name="xpad")
         nc.sync.dma_start(xpad[:, :, X0 : X0 + N], x_blocks)
-        bias_rows = held.tile([2 * NB, P], F32, name="bias_rows")
+        bias = held.tile([P, 2 * NB], F32, name="bias")
         offsets = held.tile([P, N // 16], U16, name="offsets")
         wq_sb, wv_sb, windows = [], [], []
         for g in range(NB // BPG):
@@ -57,8 +58,8 @@ def tile_slidingwindowattention_s_kernel(tc, x, wq, bq, wv, bv, base, offs, out)
             nc.sync.dma_start(wq_g[:], wq_blocks[:, :, g * GC : (g + 1) * GC])
             wq_sb.append(wq_g)
             if g == 0:
-                nc.sync.dma_start(bias_rows[0:NB, :], bq.rearrange("(b p) o -> b (p o)", p=P))
-                nc.sync.dma_start(bias_rows[NB : 2 * NB, :], bv.rearrange("(b p) o -> b (p o)", p=P))
+                nc.sync.dma_start(bias[:, 0:NB], bq.rearrange("(b p) o -> p (b o)", p=P))
+                nc.sync.dma_start(bias[:, NB : 2 * NB], bv.rearrange("(b p) o -> p (b o)", p=P))
             wv_g = held.tile([P, NB, GC], BF16, name=f"wv{g}")
             nc.sync.dma_start(wv_g[:], wv_blocks[:, :, g * GC : (g + 1) * GC])
             wv_sb.append(wv_g)
@@ -82,10 +83,6 @@ def tile_slidingwindowattention_s_kernel(tc, x, wq, bq, wv, bv, base, offs, out)
 
         ident = held.tile([P, P], F32, name="ident")
         make_identity(nc, ident[:])
-        bias_ps = psum_back.tile([P, 2 * NB], F32, name="bias_ps", tag="back_ps")
-        nc.tensor.matmul(bias_ps[:], lhsT=bias_rows[:], rhs=ident[0 : 2 * NB, 0 : 2 * NB], start=True, stop=True)
-        bias = held.tile([P, 2 * NB], F32, name="bias")
-        nc.vector.tensor_copy(bias[:], bias_ps[:])
 
         e_tiles = []
         for i in range(E_BUFS):
@@ -122,43 +119,48 @@ def tile_slidingwindowattention_s_kernel(tc, x, wq, bq, wv, bv, base, offs, out)
                 in0=v_ps[:].unsqueeze(1).to_broadcast([P, T, VROW]), scalar=bias[:, NB + b : NB + b + 1],
                 in1=e_tile[:, 0 : T * VROW].rearrange("p (t i) -> p t i", i=VROW), op0=ADD, op1=MULT)
             weighed = weighed_tile[:].rearrange("p (t r) -> p t r", r=EROW)[:, :, 0:N]
+            adder = nc.gpsimd if b < NB - VECTOR_ADDS else nc.vector
             pairs = work.tile([P, 2, N], F32, name="pairs")
-            nc.gpsimd.tensor_tensor(pairs[:], weighed[:, 0:2, :], weighed[:, 2:4, :], ADD)
+            adder.tensor_tensor(pairs[:], weighed[:, 0:2, :], weighed[:, 2:4, :], ADD)
             four = work.tile([P, N], F32, name="four")
-            nc.gpsimd.tensor_tensor(four[:], pairs[:, 0, :], pairs[:, 1, :], ADD)
-            num = kept.tile([P, N], F32, name="num")
-            nc.gpsimd.tensor_tensor(num[:], four[:], weighed[:, 4, :], ADD)
+            adder.tensor_tensor(four[:], pairs[:, 0, :], pairs[:, 1, :], ADD)
+            num = held.tile([P, N], F32, name=f"num{b}")
+            adder.tensor_tensor(num[:], four[:], weighed[:, 4, :], ADD)
             num_of[b] = num
 
         def add_den(b):
-            if b % HALF == 0:
-                den_flipped_of[b // HALF] = psum_flipped.tile([P, HALF, P], F32, name="den_flipped")
-            for t in range(T):
-                nc.tensor.matmul(den_flipped_of[b // HALF][:, b % HALF, :],
-                                 lhsT=e_of[b][:, t * EROW : t * EROW + N], rhs=ident[:],
-                                 is_transpose=True, start=(t == 0), stop=(t == T - 1))
+            for i, blocks in enumerate(DEN_TILES):
+                if b == blocks[0]:
+                    den_flipped_of[i] = psum_flipped.tile([P, len(blocks), P], F32, name="den_flipped")
+                if b in blocks:
+                    for t in range(T):
+                        nc.tensor.matmul(den_flipped_of[i][:, b - blocks[0], :],
+                                         lhsT=e_of[b][:, t * EROW : t * EROW + N], rhs=ident[:],
+                                         is_transpose=True, start=(t == 0), stop=(t == T - 1))
 
-        def invert(h):
-            root_flipped = work.tile([P, HALF, P], F32, name="root_flipped")
-            nc.scalar.activation(root_flipped[:], den_flipped_of[h][:], ABS_RSQRT)
-            for i in range(HALF):
+        def invert(i):
+            blocks = DEN_TILES[i]
+            root_flipped = work.tile([P, len(blocks), P], F32, name="root_flipped")
+            nc.scalar.activation(root_flipped[:], den_flipped_of[i][:], ABS_RSQRT)
+            for b in blocks:
                 back_ps = psum_back.tile([P, N], F32, name="back_ps")
-                nc.tensor.transpose(back_ps[:], root_flipped[:, i, :], ident[:])
-                rden = kept.tile([P, N], F32, name="rden")
+                nc.tensor.transpose(back_ps[:], root_flipped[:, b - blocks[0], :], ident[:])
+                rden = held.tile([P, N], F32, name=f"rden{b}")
                 nc.scalar.activation(rden[:], back_ps[:], SQUARE)
-                rden_of[h * HALF + i] = rden
+                rden_of[b] = rden
 
         def place(b):
             nc.vector.tensor_tensor(windows[b][:].indirect(offsets[:]), num_of[b][:], rden_of[b][:], MULT)
             nc.sync.dma_start(out[b * P : (b + 1) * P, :], windows[b][:])
 
-        for i in range(NB + 5):
-            if i < NB:
-                score(i)
-            if 0 <= i - 1 < NB:
-                weigh(i - 1)
-                add_den(i - 1)
-                if i % HALF == 0:
-                    invert((i - 1) // HALF)
-            if 0 <= i - 5 < NB:
-                place(i - 5)
+        for b in range(NB + 1):
+            if b < NB:
+                score(b)
+            if b >= 1:
+                weigh(b - 1)
+                add_den(b - 1)
+                for i in range(len(DEN_TILES)):
+                    if INVERT_AFTER[i] == b - 1:
+                        invert(i)
+        for b in range(NB):
+            place(b)

@@ -19,14 +19,14 @@ T = 2 * W + 1
 NB = C // P
 GC = 256
 BPG = GC // P
-DEN_TILES = ((0, 1, 2, 3), (4, 5, 6, 7))
-INVERT_AFTER = (3, 7)
+DEN_TILES = ((0, 2, 4, 6), (1, 3, 5, 7))
 VECTOR_ADDS = 2
 X0 = 16
 XROW = 160
 VROW = N + 2 * W
 EROW = VROW + 1
-E_BUFS = 4
+PAIR = 2
+AHEAD = 1
 XREP = 672
 WARM_COLS = 512
 WARM_MATMULS = 4
@@ -53,16 +53,18 @@ def tile_slidingwindowattention_s_kernel(tc, x, wq, bq, wv, bv, base, offs, out)
         bias = held.tile([P, 2 * NB], F32, name="bias")
         offsets = held.tile([P, N // 16], U16, name="offsets")
         wq_sb, wv_sb, windows = [], [], []
-        for g in range(NB // BPG):
-            wq_g = held.tile([P, NB, GC], BF16, name=f"wq{g}")
-            nc.sync.dma_start(wq_g[:], wq_blocks[:, :, g * GC : (g + 1) * GC])
-            wq_sb.append(wq_g)
+        for g in range(NB // BPG + AHEAD):
+            if g < NB // BPG:
+                wq_g = held.tile([P, NB, GC], BF16, name=f"wq{g}")
+                nc.sync.dma_start(wq_g[:], wq_blocks[:, :, g * GC : (g + 1) * GC])
+                wq_sb.append(wq_g)
             if g == 0:
                 nc.sync.dma_start(bias[:, 0:NB], bq.rearrange("(b p) o -> p (b o)", p=P))
                 nc.sync.dma_start(bias[:, NB : 2 * NB], bv.rearrange("(b p) o -> p (b o)", p=P))
-            wv_g = held.tile([P, NB, GC], BF16, name=f"wv{g}")
-            nc.sync.dma_start(wv_g[:], wv_blocks[:, :, g * GC : (g + 1) * GC])
-            wv_sb.append(wv_g)
+            if g >= AHEAD:
+                wv_g = held.tile([P, NB, GC], BF16, name=f"wv{g - AHEAD}")
+                nc.sync.dma_start(wv_g[:], wv_blocks[:, :, (g - AHEAD) * GC : (g - AHEAD + 1) * GC])
+                wv_sb.append(wv_g)
         nc.sync.dma_start(offsets[:], offs)
         for b in range(NB):
             window = held.tile([P, S], F32, name=f"window{b}")
@@ -84,13 +86,13 @@ def tile_slidingwindowattention_s_kernel(tc, x, wq, bq, wv, bv, base, offs, out)
         ident = held.tile([P, P], F32, name="ident")
         make_identity(nc, ident[:])
 
-        e_tiles = []
-        for i in range(E_BUFS):
-            e_tile = held.tile([P, T * EROW], F32, name=f"e{i}")
-            nc.vector.memset(e_tile[:].rearrange("p (t r) -> p t r", r=EROW)[:, :, N:EROW], 0.0)
-            e_tiles.append(e_tile)
+        e_pairs = []
+        for i in range(NB // PAIR):
+            e_pair = held.tile([P, PAIR, T * EROW], F32, name=f"e{i}")
+            nc.vector.memset(e_pair[:].rearrange("p h (t r) -> p h t r", r=EROW)[:, :, :, N:EROW], 0.0)
+            e_pairs.append(e_pair)
 
-        v_of, e_of, num_of, den_flipped_of, rden_of = {}, {}, {}, {}, {}
+        scores_of, e_of, num_of, den_flipped_of, rden_of = {}, {}, {}, {}, {}
 
         def score(b):
             g, cols = b // BPG, slice((b % BPG) * P, (b % BPG + 1) * P)
@@ -98,21 +100,25 @@ def tile_slidingwindowattention_s_kernel(tc, x, wq, bq, wv, bv, base, offs, out)
             for k in range(NB):
                 nc.tensor.matmul(q_ps[:], lhsT=wq_sb[g][:, k, cols], rhs=xpad[:, k, X0 : X0 + N],
                                  start=(k == 0), stop=(k == NB - 1))
+            if b % PAIR == 0:
+                scores_of[b // PAIR] = work.tile([P, PAIR, T, N], F32, name="scores")
+            scores = scores_of[b // PAIR]
+            nc.vector.scalar_tensor_tensor(
+                out=scores[:, b % PAIR, :, :], in0=q_ps[:].unsqueeze(1).to_broadcast([P, T, N]),
+                scalar=bias[:, b : b + 1],
+                in1=xrep[:, b, 0 : T * EROW].rearrange("p (t r) -> p t r", r=EROW)[:, :, 0:N], op0=ADD, op1=MULT)
+            e_pair = e_pairs[b // PAIR]
+            if b % PAIR == PAIR - 1:
+                nc.scalar.activation(e_pair[:].rearrange("p h (t r) -> p h t r", r=EROW)[:, :, :, 0:N], scores[:], EXP)
+            e_of[b] = e_pair[:, b % PAIR, :]
+
+        def weigh(b):
+            g, cols = b // BPG, slice((b % BPG) * P, (b % BPG + 1) * P)
             v_ps = psum_v.tile([P, N + 2 * W], F32, name="v_ps")
             for k in range(NB):
                 nc.tensor.matmul(v_ps[:], lhsT=wv_sb[g][:, k, cols], rhs=xpad[:, k, X0 - W : X0 + N + W],
                                  start=(k == 0), stop=(k == NB - 1))
-            scores = work.tile([P, T, N], F32, name="scores")
-            nc.vector.scalar_tensor_tensor(
-                out=scores[:], in0=q_ps[:].unsqueeze(1).to_broadcast([P, T, N]), scalar=bias[:, b : b + 1],
-                in1=xrep[:, b, 0 : T * EROW].rearrange("p (t r) -> p t r", r=EROW)[:, :, 0:N], op0=ADD, op1=MULT)
-            e_tile = e_tiles[b % E_BUFS]
-            e = e_tile[:].rearrange("p (t r) -> p t r", r=EROW)[:, :, 0:N]
-            nc.scalar.activation(e, scores[:], EXP)
-            v_of[b], e_of[b] = v_ps, e_tile
-
-        def weigh(b):
-            v_ps, e_tile = v_of[b], e_of[b]
+            e_tile = e_of[b]
             weighed_tile = work.tile([P, T * EROW], F32, name="weighed_tile")
             nc.vector.scalar_tensor_tensor(
                 out=weighed_tile[:, 0 : T * VROW].rearrange("p (t i) -> p t i", i=VROW),
@@ -134,7 +140,7 @@ def tile_slidingwindowattention_s_kernel(tc, x, wq, bq, wv, bv, base, offs, out)
                     den_flipped_of[i] = psum_flipped.tile([P, len(blocks), P], F32, name="den_flipped")
                 if b in blocks:
                     for t in range(T):
-                        nc.tensor.matmul(den_flipped_of[i][:, b - blocks[0], :],
+                        nc.tensor.matmul(den_flipped_of[i][:, blocks.index(b), :],
                                          lhsT=e_of[b][:, t * EROW : t * EROW + N], rhs=ident[:],
                                          is_transpose=True, start=(t == 0), stop=(t == T - 1))
 
@@ -144,7 +150,7 @@ def tile_slidingwindowattention_s_kernel(tc, x, wq, bq, wv, bv, base, offs, out)
             nc.scalar.activation(root_flipped[:], den_flipped_of[i][:], ABS_RSQRT)
             for b in blocks:
                 back_ps = psum_back.tile([P, N], F32, name="back_ps")
-                nc.tensor.transpose(back_ps[:], root_flipped[:, b - blocks[0], :], ident[:])
+                nc.tensor.transpose(back_ps[:], root_flipped[:, blocks.index(b), :], ident[:])
                 rden = held.tile([P, N], F32, name=f"rden{b}")
                 nc.scalar.activation(rden[:], back_ps[:], SQUARE)
                 rden_of[b] = rden
@@ -153,14 +159,16 @@ def tile_slidingwindowattention_s_kernel(tc, x, wq, bq, wv, bv, base, offs, out)
             nc.vector.tensor_tensor(windows[b][:].indirect(offsets[:]), num_of[b][:], rden_of[b][:], MULT)
             nc.sync.dma_start(out[b * P : (b + 1) * P, :], windows[b][:])
 
-        for b in range(NB + 1):
-            if b < NB:
-                score(b)
-            if b >= 1:
-                weigh(b - 1)
-                add_den(b - 1)
-                for i in range(len(DEN_TILES)):
-                    if INVERT_AFTER[i] == b - 1:
-                        invert(i)
+        lead = (1 + AHEAD) * PAIR
+        for first in range(0, NB + lead, PAIR):
+            for b in range(first, first + PAIR):
+                if b < NB:
+                    score(b)
+            for b in range(first - lead, first - lead + PAIR):
+                if b >= 0:
+                    weigh(b)
+                    add_den(b)
+        for i in range(len(DEN_TILES)):
+            invert(i)
         for b in range(NB):
             place(b)

@@ -17,7 +17,7 @@ S = 256
 W = 2
 T = 2 * W + 1
 NB = C // P
-GC = 256
+GC = 512
 BPG = GC // P
 DEN_TILES = ((0, 2, 4, 6), (1, 3, 5, 7))
 VECTOR_ADDS = 2
@@ -26,7 +26,7 @@ XROW = 160
 VROW = N + 2 * W
 EROW = VROW + 1
 PAIR = 2
-AHEAD = 1
+AHEAD = 0
 XREP = 672
 WARM_COLS = 512
 WARM_MATMULS = 4

@@ -17,21 +17,25 @@ S = 256
 W = 2
 T = 2 * W + 1
 NB = C // P
-GC = 512
-BPG = GC // P
-DEN_TILES = ((0, 2, 4, 6), (1, 3, 5, 7))
-VECTOR_ADDS = 2
+LOAD_BLOCKS = 4
+PAIR = 2
+BANKS = 2
+VECTOR_SUMS = 2
 X0 = 16
 XROW = 160
-VROW = N + 2 * W
-EROW = VROW + 1
-PAIR = 2
-AHEAD = 0
+KEYS = N + 2 * W
+STEP = KEYS + 1
 XREP = 672
-WARM_COLS = 512
-WARM_MATMULS = 4
 
 FLOPS = 2 * 2 * C * C * N
+
+
+def by_query(rows):
+    return rows[:, 0 : T * STEP].rearrange("p (t s) -> p t s", s=STEP)[:, :, 0:N]
+
+
+def by_key(rows):
+    return rows[:, 0 : T * KEYS].rearrange("p (t k) -> p t k", k=KEYS)
 
 
 def tile_slidingwindowattention_s_kernel(tc, x, wq, bq, wv, bv, base, offs, out):
@@ -39,118 +43,104 @@ def tile_slidingwindowattention_s_kernel(tc, x, wq, bq, wv, bv, base, offs, out)
     x_blocks = x.rearrange("(b p) j -> p b j", p=P)
     wq_blocks = wq.rearrange("(k p) c -> p k c", p=P)
     wv_blocks = wv.rearrange("(k p) c -> p k c", p=P)
+    load_cols = LOAD_BLOCKS * P
 
     with (
         tc.tile_pool(name="held", bufs=1) as held,
         tc.tile_pool(name="work", bufs=4) as work,
         tc.psum_pool(name="psum_q", bufs=2) as psum_q,
         tc.psum_pool(name="psum_v", bufs=2) as psum_v,
-        tc.psum_pool(name="psum_flipped", bufs=2) as psum_flipped,
+        tc.psum_pool(name="psum_flipped", bufs=BANKS) as psum_flipped,
         tc.psum_pool(name="psum_back", bufs=2) as psum_back,
     ):
         xpad = held.tile([P, NB, XROW], BF16, name="xpad")
         nc.sync.dma_start(xpad[:, :, X0 : X0 + N], x_blocks)
         bias = held.tile([P, 2 * NB], F32, name="bias")
         offsets = held.tile([P, N // 16], U16, name="offsets")
-        wq_sb, wv_sb, windows = [], [], []
-        for g in range(NB // BPG + AHEAD):
-            if g < NB // BPG:
-                wq_g = held.tile([P, NB, GC], BF16, name=f"wq{g}")
-                nc.sync.dma_start(wq_g[:], wq_blocks[:, :, g * GC : (g + 1) * GC])
-                wq_sb.append(wq_g)
+        wq_loads, wv_loads, windows = [], [], []
+        for g in range(NB // LOAD_BLOCKS):
+            wq_load = held.tile([P, NB, load_cols], BF16, name=f"wq{g}")
+            nc.sync.dma_start(wq_load[:], wq_blocks[:, :, g * load_cols : (g + 1) * load_cols])
+            wq_loads.append(wq_load)
             if g == 0:
                 nc.sync.dma_start(bias[:, 0:NB], bq.rearrange("(b p) o -> p (b o)", p=P))
                 nc.sync.dma_start(bias[:, NB : 2 * NB], bv.rearrange("(b p) o -> p (b o)", p=P))
-            if g >= AHEAD:
-                wv_g = held.tile([P, NB, GC], BF16, name=f"wv{g - AHEAD}")
-                nc.sync.dma_start(wv_g[:], wv_blocks[:, :, (g - AHEAD) * GC : (g - AHEAD + 1) * GC])
-                wv_sb.append(wv_g)
+            wv_load = held.tile([P, NB, load_cols], BF16, name=f"wv{g}")
+            nc.sync.dma_start(wv_load[:], wv_blocks[:, :, g * load_cols : (g + 1) * load_cols])
+            wv_loads.append(wv_load)
         nc.sync.dma_start(offsets[:], offs)
         for b in range(NB):
             window = held.tile([P, S], F32, name=f"window{b}")
             nc.sync.dma_start(window[:], base[b * P : (b + 1) * P, :])
             windows.append(window)
 
-        zeros = held.tile([P, WARM_COLS], BF16, name="zeros")
-        nc.vector.memset(zeros[:], 0.0)
-        warm_ps = psum_back.tile([P, WARM_COLS], F32, name="warm_ps", tag="back_ps")
-        for i in range(WARM_MATMULS):
-            nc.tensor.matmul(warm_ps[:], lhsT=zeros[:, 0:P], rhs=zeros[:], start=True, stop=True)
-
         nc.vector.tensor_copy(xpad[:, :, X0 - W : X0], xpad[:, :, X0 + N - W : X0 + N])
         nc.vector.tensor_copy(xpad[:, :, X0 + N : X0 + N + W], xpad[:, :, X0 : X0 + W])
         xrep = held.tile([P, NB, XREP], BF16, name="xrep")
         for t in range(T):
-            nc.vector.tensor_copy(xrep[:, :, t * VROW : (t + 1) * VROW], xpad[:, :, X0 - W : X0 + N + W])
+            nc.vector.tensor_copy(xrep[:, :, t * KEYS : (t + 1) * KEYS], xpad[:, :, X0 - W : X0 + N + W])
 
         ident = held.tile([P, P], F32, name="ident")
         make_identity(nc, ident[:])
 
         e_pairs = []
         for i in range(NB // PAIR):
-            e_pair = held.tile([P, PAIR, T * EROW], F32, name=f"e{i}")
-            nc.vector.memset(e_pair[:].rearrange("p h (t r) -> p h t r", r=EROW)[:, :, :, N:EROW], 0.0)
+            e_pair = held.tile([P, PAIR, T * STEP], F32, name=f"e{i}")
+            nc.vector.memset(e_pair[:].rearrange("p h (t s) -> p h t s", s=STEP)[:, :, :, N:STEP], 0.0)
             e_pairs.append(e_pair)
 
         scores_of, e_of, num_of, den_flipped_of, rden_of = {}, {}, {}, {}, {}
 
-        def score(b):
-            g, cols = b // BPG, slice((b % BPG) * P, (b % BPG + 1) * P)
-            q_ps = psum_q.tile([P, N], F32, name="q_ps")
+        def project(psum_pool, name, loads, b, first, last):
+            w_block = loads[b // LOAD_BLOCKS][:, :, (b % LOAD_BLOCKS) * P : (b % LOAD_BLOCKS + 1) * P]
+            product = psum_pool.tile([P, last - first], F32, name=name)
             for k in range(NB):
-                nc.tensor.matmul(q_ps[:], lhsT=wq_sb[g][:, k, cols], rhs=xpad[:, k, X0 : X0 + N],
+                nc.tensor.matmul(product[:], lhsT=w_block[:, k, :], rhs=xpad[:, k, first:last],
                                  start=(k == 0), stop=(k == NB - 1))
+            return product
+
+        def score(b):
+            q_ps = project(psum_q, "q_ps", wq_loads, b, X0, X0 + N)
             if b % PAIR == 0:
                 scores_of[b // PAIR] = work.tile([P, PAIR, T, N], F32, name="scores")
             scores = scores_of[b // PAIR]
             nc.vector.scalar_tensor_tensor(
                 out=scores[:, b % PAIR, :, :], in0=q_ps[:].unsqueeze(1).to_broadcast([P, T, N]),
-                scalar=bias[:, b : b + 1],
-                in1=xrep[:, b, 0 : T * EROW].rearrange("p (t r) -> p t r", r=EROW)[:, :, 0:N], op0=ADD, op1=MULT)
+                scalar=bias[:, b : b + 1], in1=by_query(xrep[:, b, :]), op0=ADD, op1=MULT)
             e_pair = e_pairs[b // PAIR]
             if b % PAIR == PAIR - 1:
-                nc.scalar.activation(e_pair[:].rearrange("p h (t r) -> p h t r", r=EROW)[:, :, :, 0:N], scores[:], EXP)
+                nc.scalar.activation(e_pair[:].rearrange("p h (t s) -> p h t s", s=STEP)[:, :, :, 0:N], scores[:], EXP)
             e_of[b] = e_pair[:, b % PAIR, :]
 
         def weigh(b):
-            g, cols = b // BPG, slice((b % BPG) * P, (b % BPG + 1) * P)
-            v_ps = psum_v.tile([P, N + 2 * W], F32, name="v_ps")
-            for k in range(NB):
-                nc.tensor.matmul(v_ps[:], lhsT=wv_sb[g][:, k, cols], rhs=xpad[:, k, X0 - W : X0 + N + W],
-                                 start=(k == 0), stop=(k == NB - 1))
-            e_tile = e_of[b]
-            weighed_tile = work.tile([P, T * EROW], F32, name="weighed_tile")
+            v_ps = project(psum_v, "v_ps", wv_loads, b, X0 - W, X0 + N + W)
+            weighed = work.tile([P, T * STEP], F32, name="weighed")
             nc.vector.scalar_tensor_tensor(
-                out=weighed_tile[:, 0 : T * VROW].rearrange("p (t i) -> p t i", i=VROW),
-                in0=v_ps[:].unsqueeze(1).to_broadcast([P, T, VROW]), scalar=bias[:, NB + b : NB + b + 1],
-                in1=e_tile[:, 0 : T * VROW].rearrange("p (t i) -> p t i", i=VROW), op0=ADD, op1=MULT)
-            weighed = weighed_tile[:].rearrange("p (t r) -> p t r", r=EROW)[:, :, 0:N]
-            adder = nc.gpsimd if b < NB - VECTOR_ADDS else nc.vector
-            pairs = work.tile([P, 2, N], F32, name="pairs")
-            adder.tensor_tensor(pairs[:], weighed[:, 0:2, :], weighed[:, 2:4, :], ADD)
+                out=by_key(weighed), in0=v_ps[:].unsqueeze(1).to_broadcast([P, T, KEYS]),
+                scalar=bias[:, NB + b : NB + b + 1], in1=by_key(e_of[b]), op0=ADD, op1=MULT)
+            rows = by_query(weighed)
+            adder = nc.gpsimd if b < NB - VECTOR_SUMS else nc.vector
+            two = work.tile([P, 2, N], F32, name="two")
+            adder.tensor_tensor(two[:], rows[:, 0:2, :], rows[:, 2:4, :], ADD)
             four = work.tile([P, N], F32, name="four")
-            adder.tensor_tensor(four[:], pairs[:, 0, :], pairs[:, 1, :], ADD)
+            adder.tensor_tensor(four[:], two[:, 0, :], two[:, 1, :], ADD)
             num = held.tile([P, N], F32, name=f"num{b}")
-            adder.tensor_tensor(num[:], four[:], weighed[:, 4, :], ADD)
+            adder.tensor_tensor(num[:], four[:], rows[:, 4, :], ADD)
             num_of[b] = num
 
         def add_den(b):
-            for i, blocks in enumerate(DEN_TILES):
-                if b == blocks[0]:
-                    den_flipped_of[i] = psum_flipped.tile([P, len(blocks), P], F32, name="den_flipped")
-                if b in blocks:
-                    for t in range(T):
-                        nc.tensor.matmul(den_flipped_of[i][:, blocks.index(b), :],
-                                         lhsT=e_of[b][:, t * EROW : t * EROW + N], rhs=ident[:],
-                                         is_transpose=True, start=(t == 0), stop=(t == T - 1))
+            if b < BANKS:
+                den_flipped_of[b] = psum_flipped.tile([P, NB // BANKS, P], F32, name="den_flipped")
+            for t in range(T):
+                nc.tensor.matmul(den_flipped_of[b % BANKS][:, b // BANKS, :], lhsT=by_query(e_of[b])[:, t, :],
+                                 rhs=ident[:], is_transpose=True, start=(t == 0), stop=(t == T - 1))
 
-        def invert(i):
-            blocks = DEN_TILES[i]
-            root_flipped = work.tile([P, len(blocks), P], F32, name="root_flipped")
-            nc.scalar.activation(root_flipped[:], den_flipped_of[i][:], ABS_RSQRT)
-            for b in blocks:
+        def invert(bank):
+            root_flipped = work.tile([P, NB // BANKS, P], F32, name="root_flipped")
+            nc.scalar.activation(root_flipped[:], den_flipped_of[bank][:], ABS_RSQRT)
+            for b in range(bank, NB, BANKS):
                 back_ps = psum_back.tile([P, N], F32, name="back_ps")
-                nc.tensor.transpose(back_ps[:], root_flipped[:, blocks.index(b), :], ident[:])
+                nc.tensor.transpose(back_ps[:], root_flipped[:, b // BANKS, :], ident[:])
                 rden = held.tile([P, N], F32, name=f"rden{b}")
                 nc.scalar.activation(rden[:], back_ps[:], SQUARE)
                 rden_of[b] = rden
@@ -159,16 +149,18 @@ def tile_slidingwindowattention_s_kernel(tc, x, wq, bq, wv, bv, base, offs, out)
             nc.vector.tensor_tensor(windows[b][:].indirect(offsets[:]), num_of[b][:], rden_of[b][:], MULT)
             nc.sync.dma_start(out[b * P : (b + 1) * P, :], windows[b][:])
 
-        lead = (1 + AHEAD) * PAIR
-        for first in range(0, NB + lead, PAIR):
+        for b in range(PAIR):
+            score(b)
+        for first in range(PAIR, NB, PAIR):
             for b in range(first, first + PAIR):
-                if b < NB:
-                    score(b)
-            for b in range(first - lead, first - lead + PAIR):
-                if b >= 0:
-                    weigh(b)
-                    add_den(b)
-        for i in range(len(DEN_TILES)):
-            invert(i)
+                score(b)
+            for b in range(first - PAIR, first):
+                weigh(b)
+                add_den(b)
+        for b in range(NB - PAIR, NB):
+            weigh(b)
+            add_den(b)
+        for bank in range(BANKS):
+            invert(bank)
         for b in range(NB):
             place(b)

@@ -64,10 +64,11 @@ def tile_slidingwindowattention_s_kernel(tc, x, wq, bq, wv, bv, base, offs, out)
             wq_loads.append(wq_load)
             if g == 0:
                 nc.sync.dma_start(bias[:, 0:NB], bq.rearrange("(b p) o -> p (b o)", p=P))
-                nc.sync.dma_start(bias[:, NB : 2 * NB], bv.rearrange("(b p) o -> p (b o)", p=P))
             wv_load = held.tile([P, NB, load_cols], BF16, name=f"wv{g}")
             nc.sync.dma_start(wv_load[:], wv_blocks[:, :, g * load_cols : (g + 1) * load_cols])
             wv_loads.append(wv_load)
+            if g == 0:
+                nc.sync.dma_start(bias[:, NB : 2 * NB], bv.rearrange("(b p) o -> p (b o)", p=P))
         nc.sync.dma_start(offsets[:], offs)
         for b in range(NB):
             window = held.tile([P, S], F32, name=f"window{b}")

@@ -20,7 +20,7 @@ NB = C // P
 LOAD_BLOCKS = 4
 PAIR = 2
 BANKS = 2
-VECTOR_SUMS = 2
+VECTOR_SUMS = 3
 X0 = 16
 XROW = 160
 KEYS = N + 2 * W

@@ -17,12 +17,11 @@ S = 256
 W = 2
 T = 2 * W + 1
 NB = C // P
-LOAD_BLOCKS = 4
+HALVES = 2
+R = NB // HALVES
 PAIR = 2
 BANKS = 2
 VECTOR_SUMS = 3
-X0 = 16
-XROW = 160
 KEYS = N + 2 * W
 STEP = KEYS + 1
 XREP = 672
@@ -40,10 +39,11 @@ def by_key(rows):
 
 def tile_slidingwindowattention_s_kernel(tc, x, wq, bq, wv, bv, base, offs, out):
     nc = tc.nc
-    x_blocks = x.rearrange("(b p) j -> p b j", p=P)
-    wq_blocks = wq.rearrange("(k p) c -> p k c", p=P)
-    wv_blocks = wv.rearrange("(k p) c -> p k c", p=P)
-    load_cols = LOAD_BLOCKS * P
+    half_cols = C // HALVES
+    wq_rows = wq.rearrange("(h p r) c -> h p r c", h=HALVES, p=P)
+    wv_rows = wv.rearrange("(h p r) c -> h p r c", h=HALVES, p=P)
+    base_rows = base.rearrange("(h p r) s -> h p r s", h=HALVES, p=P)
+    out_rows = out.rearrange("(h p r) s -> h p r s", h=HALVES, p=P)
 
     with (
         tc.tile_pool(name="held", bufs=1) as held,
@@ -53,33 +53,41 @@ def tile_slidingwindowattention_s_kernel(tc, x, wq, bq, wv, bv, base, offs, out)
         tc.psum_pool(name="psum_flipped", bufs=BANKS) as psum_flipped,
         tc.psum_pool(name="psum_back", bufs=2) as psum_back,
     ):
-        xpad = held.tile([P, NB, XROW], BF16, name="xpad")
-        nc.sync.dma_start(xpad[:, :, X0 : X0 + N], x_blocks)
+        xt = held.tile([P, NB, N], BF16, name="xt")
+        nc.sync.dma_start(xt[:].rearrange("p (h r) j -> p h (r j)", h=HALVES),
+                          x.rearrange("(h p r) j -> p h (r j)", h=HALVES, p=P))
         bias = held.tile([P, 2 * NB], F32, name="bias")
         offsets = held.tile([P, N // 16], U16, name="offsets")
-        wq_loads, wv_loads, windows = [], [], []
-        for g in range(NB // LOAD_BLOCKS):
-            wq_load = held.tile([P, NB, load_cols], BF16, name=f"wq{g}")
-            nc.sync.dma_start(wq_load[:], wq_blocks[:, :, g * load_cols : (g + 1) * load_cols])
-            wq_loads.append(wq_load)
-            if g == 0:
-                nc.sync.dma_start(bias[:, 0:NB], bq.rearrange("(b p) o -> p (b o)", p=P))
-            wv_load = held.tile([P, NB, load_cols], BF16, name=f"wv{g}")
-            nc.sync.dma_start(wv_load[:], wv_blocks[:, :, g * load_cols : (g + 1) * load_cols])
-            wv_loads.append(wv_load)
-            if g == 0:
-                nc.sync.dma_start(bias[:, NB : 2 * NB], bv.rearrange("(b p) o -> p (b o)", p=P))
+        wq_loads, wv_loads, windows = {}, {}, []
+
+        def load_weights(name, loads, rows, half):
+            for k_half in range(HALVES):
+                loads[half, k_half] = held.tile([P, R, half_cols], BF16, name=f"{name}{half}{k_half}")
+                nc.sync.dma_start(loads[half, k_half][:],
+                                  rows[k_half][:, :, half * half_cols : (half + 1) * half_cols])
+
+        def load_bias(column, bias_dram):
+            nc.sync.dma_start(bias[:, column : column + NB].rearrange("p (h r) -> p h r", h=HALVES),
+                              bias_dram.rearrange("(h p r) o -> p h (r o)", h=HALVES, p=P))
+
+        load_weights("wq", wq_loads, wq_rows, 0)
+        load_bias(0, bq)
+        load_weights("wv", wv_loads, wv_rows, 0)
+        load_bias(NB, bv)
+        load_weights("wq", wq_loads, wq_rows, 1)
+        load_weights("wv", wv_loads, wv_rows, 1)
         nc.sync.dma_start(offsets[:], offs)
         for b in range(NB):
             window = held.tile([P, S], F32, name=f"window{b}")
-            nc.sync.dma_start(window[:], base[b * P : (b + 1) * P, :])
+            nc.sync.dma_start(window[:], base_rows[b // R][:, b % R, :])
             windows.append(window)
 
-        nc.vector.tensor_copy(xpad[:, :, X0 - W : X0], xpad[:, :, X0 + N - W : X0 + N])
-        nc.vector.tensor_copy(xpad[:, :, X0 + N : X0 + N + W], xpad[:, :, X0 : X0 + W])
         xrep = held.tile([P, NB, XREP], BF16, name="xrep")
-        for t in range(T):
-            nc.vector.tensor_copy(xrep[:, :, t * KEYS : (t + 1) * KEYS], xpad[:, :, X0 - W : X0 + N + W])
+        nc.vector.tensor_copy(xrep[:, :, W : W + N], xt[:])
+        nc.vector.tensor_copy(xrep[:, :, 0:W], xt[:, :, N - W : N])
+        nc.vector.tensor_copy(xrep[:, :, W + N : KEYS], xt[:, :, 0:W])
+        for t in range(1, T):
+            nc.vector.tensor_copy(xrep[:, :, t * KEYS : (t + 1) * KEYS], xrep[:, :, 0:KEYS])
 
         ident = held.tile([P, P], F32, name="ident")
         make_identity(nc, ident[:])
@@ -92,16 +100,16 @@ def tile_slidingwindowattention_s_kernel(tc, x, wq, bq, wv, bv, base, offs, out)
 
         scores_of, e_of, num_of, den_flipped_of, rden_of = {}, {}, {}, {}, {}
 
-        def project(psum_pool, name, loads, b, first, last):
-            w_block = loads[b // LOAD_BLOCKS][:, :, (b % LOAD_BLOCKS) * P : (b % LOAD_BLOCKS + 1) * P]
-            product = psum_pool.tile([P, last - first], F32, name=name)
+        def project(psum_pool, name, loads, b, x_rows):
+            product = psum_pool.tile([P, x_rows.shape[2]], F32, name=name)
             for k in range(NB):
-                nc.tensor.matmul(product[:], lhsT=w_block[:, k, :], rhs=xpad[:, k, first:last],
+                w_rows = loads[b // R, k // R][:].rearrange("p k (m r) -> p k r m", r=R)
+                nc.tensor.matmul(product[:], lhsT=w_rows[:, k % R, b % R, :], rhs=x_rows[:, k, :],
                                  start=(k == 0), stop=(k == NB - 1))
             return product
 
         def score(b):
-            q_ps = project(psum_q, "q_ps", wq_loads, b, X0, X0 + N)
+            q_ps = project(psum_q, "q_ps", wq_loads, b, xt[:])
             if b % PAIR == 0:
                 scores_of[b // PAIR] = work.tile([P, PAIR, T, N], F32, name="scores")
             scores = scores_of[b // PAIR]
@@ -114,7 +122,7 @@ def tile_slidingwindowattention_s_kernel(tc, x, wq, bq, wv, bv, base, offs, out)
             e_of[b] = e_pair[:, b % PAIR, :]
 
         def weigh(b):
-            v_ps = project(psum_v, "v_ps", wv_loads, b, X0 - W, X0 + N + W)
+            v_ps = project(psum_v, "v_ps", wv_loads, b, xrep[:, :, 0:KEYS])
             weighed = work.tile([P, T * STEP], F32, name="weighed")
             nc.vector.scalar_tensor_tensor(
                 out=by_key(weighed), in0=v_ps[:].unsqueeze(1).to_broadcast([P, T, KEYS]),
@@ -148,7 +156,7 @@ def tile_slidingwindowattention_s_kernel(tc, x, wq, bq, wv, bv, base, offs, out)
 
         def place(b):
             nc.vector.tensor_tensor(windows[b][:].indirect(offsets[:]), num_of[b][:], rden_of[b][:], MULT)
-            nc.sync.dma_start(out[b * P : (b + 1) * P, :], windows[b][:])
+            nc.sync.dma_start(out_rows[b // R][:, b % R, :], windows[b][:])
 
         for b in range(PAIR):
             score(b)

@@ -9,6 +9,7 @@ MULT = mybir.AluOpType.mult
 EXP = mybir.ActivationFunctionType.Exp
 ABS_RSQRT = mybir.ActivationFunctionType.Abs_reciprocal_sqrt
 SQUARE = mybir.ActivationFunctionType.Square
+COPY = mybir.ActivationFunctionType.Copy
 
 P = 128
 C = 1024
@@ -20,8 +21,6 @@ NB = C // P
 HALVES = 2
 R = NB // HALVES
 PAIR = 2
-BANKS = 2
-VECTOR_SUMS = 3
 KEYS = N + 2 * W
 STEP = KEYS + 1
 XREP = 672
@@ -48,10 +47,8 @@ def tile_slidingwindowattention_s_kernel(tc, x, wq, bq, wv, bv, base, offs, out)
     with (
         tc.tile_pool(name="held", bufs=1) as held,
         tc.tile_pool(name="work", bufs=4) as work,
-        tc.psum_pool(name="psum_q", bufs=2) as psum_q,
-        tc.psum_pool(name="psum_v", bufs=2) as psum_v,
-        tc.psum_pool(name="psum_flipped", bufs=BANKS) as psum_flipped,
-        tc.psum_pool(name="psum_back", bufs=2) as psum_back,
+        tc.psum_pool(name="psum_ring", bufs=6) as psum_ring,
+        tc.psum_pool(name="psum_flipped", bufs=HALVES) as psum_flipped,
     ):
         xt = held.tile([P, NB, N], BF16, name="xt")
         nc.sync.dma_start(xt[:].rearrange("p (h r) j -> p h (r j)", h=HALVES),
@@ -72,9 +69,9 @@ def tile_slidingwindowattention_s_kernel(tc, x, wq, bq, wv, bv, base, offs, out)
 
         load_weights("wq", wq_loads, wq_rows, 0)
         load_bias(0, bq)
+        load_weights("wq", wq_loads, wq_rows, 1)
         load_weights("wv", wv_loads, wv_rows, 0)
         load_bias(NB, bv)
-        load_weights("wq", wq_loads, wq_rows, 1)
         load_weights("wv", wv_loads, wv_rows, 1)
         nc.sync.dma_start(offsets[:], offs)
         for b in range(NB):
@@ -98,10 +95,10 @@ def tile_slidingwindowattention_s_kernel(tc, x, wq, bq, wv, bv, base, offs, out)
             nc.vector.memset(e_pair[:].rearrange("p h (t s) -> p h t s", s=STEP)[:, :, :, N:STEP], 0.0)
             e_pairs.append(e_pair)
 
-        scores_of, e_of, num_of, den_flipped_of, rden_of = {}, {}, {}, {}, {}
+        scores_of, e_of, weighed_of, num_of, den_flipped_of, rden_of = {}, {}, {}, {}, {}, {}
 
-        def project(psum_pool, name, loads, b, x_rows):
-            product = psum_pool.tile([P, x_rows.shape[2]], F32, name=name)
+        def project(name, loads, b, x_rows):
+            product = psum_ring.tile([P, x_rows.shape[2]], F32, name=name, tag="ring")
             for k in range(NB):
                 w_rows = loads[b // R, k // R][:].rearrange("p k (m r) -> p k r m", r=R)
                 nc.tensor.matmul(product[:], lhsT=w_rows[:, k % R, b % R, :], rhs=x_rows[:, k, :],
@@ -109,7 +106,7 @@ def tile_slidingwindowattention_s_kernel(tc, x, wq, bq, wv, bv, base, offs, out)
             return product
 
         def score(b):
-            q_ps = project(psum_q, "q_ps", wq_loads, b, xt[:])
+            q_ps = project("q_ps", wq_loads, b, xt[:])
             if b % PAIR == 0:
                 scores_of[b // PAIR] = work.tile([P, PAIR, T, N], F32, name="scores")
             scores = scores_of[b // PAIR]
@@ -122,34 +119,43 @@ def tile_slidingwindowattention_s_kernel(tc, x, wq, bq, wv, bv, base, offs, out)
             e_of[b] = e_pair[:, b % PAIR, :]
 
         def weigh(b):
-            v_ps = project(psum_v, "v_ps", wv_loads, b, xrep[:, :, 0:KEYS])
-            weighed = work.tile([P, T * STEP], F32, name="weighed")
+            v_ps = project("v_ps", wv_loads, b, xrep[:, :, 0:KEYS])
+            weighed = held.tile([P, T * STEP], F32, name=f"weighed{b}")
             nc.vector.scalar_tensor_tensor(
                 out=by_key(weighed), in0=v_ps[:].unsqueeze(1).to_broadcast([P, T, KEYS]),
                 scalar=bias[:, NB + b : NB + b + 1], in1=by_key(e_of[b]), op0=ADD, op1=MULT)
-            rows = by_query(weighed)
-            adder = nc.gpsimd if b < NB - VECTOR_SUMS else nc.vector
+            weighed_of[b] = weighed
+
+        def add_num(engine, b):
+            rows = by_query(weighed_of[b])
             two = work.tile([P, 2, N], F32, name="two")
-            adder.tensor_tensor(two[:], rows[:, 0:2, :], rows[:, 2:4, :], ADD)
+            engine.tensor_tensor(two[:], rows[:, 0:2, :], rows[:, 2:4, :], ADD)
             four = work.tile([P, N], F32, name="four")
-            adder.tensor_tensor(four[:], two[:, 0, :], two[:, 1, :], ADD)
-            num = held.tile([P, N], F32, name=f"num{b}")
-            adder.tensor_tensor(num[:], four[:], rows[:, 4, :], ADD)
-            num_of[b] = num
+            engine.tensor_tensor(four[:], two[:, 0, :], two[:, 1, :], ADD)
+            num_of[b] = held.tile([P, N], F32, name=f"num{b}")
+            engine.tensor_tensor(num_of[b][:], four[:], rows[:, 4, :], ADD)
+
+        def add_num_on_tensor(b):
+            num_ps = psum_ring.tile([P, N], F32, name="num_ps", tag="ring")
+            for t in range(T):
+                nc.tensor.matmul(num_ps[:], lhsT=ident[:], rhs=by_query(weighed_of[b])[:, t, :],
+                                 start=(t == 0), stop=(t == T - 1))
+            num_of[b] = held.tile([P, N], F32, name=f"num{b}")
+            nc.scalar.activation(num_of[b][:], num_ps[:], COPY)
 
         def add_den(b):
-            if b < BANKS:
-                den_flipped_of[b] = psum_flipped.tile([P, NB // BANKS, P], F32, name="den_flipped")
+            if b % R == 0:
+                den_flipped_of[b // R] = psum_flipped.tile([P, R, P], F32, name="den_flipped")
             for t in range(T):
-                nc.tensor.matmul(den_flipped_of[b % BANKS][:, b // BANKS, :], lhsT=by_query(e_of[b])[:, t, :],
+                nc.tensor.matmul(den_flipped_of[b // R][:, b % R, :], lhsT=by_query(e_of[b])[:, t, :],
                                  rhs=ident[:], is_transpose=True, start=(t == 0), stop=(t == T - 1))
 
-        def invert(bank):
-            root_flipped = work.tile([P, NB // BANKS, P], F32, name="root_flipped")
-            nc.scalar.activation(root_flipped[:], den_flipped_of[bank][:], ABS_RSQRT)
-            for b in range(bank, NB, BANKS):
-                back_ps = psum_back.tile([P, N], F32, name="back_ps")
-                nc.tensor.transpose(back_ps[:], root_flipped[:, b // BANKS, :], ident[:])
+        def invert(half):
+            root_flipped = scores_of[NB // PAIR - 1][:, half, 0:R, :]
+            nc.scalar.activation(root_flipped, den_flipped_of[half][:], ABS_RSQRT)
+            for b in range(half * R, (half + 1) * R):
+                back_ps = psum_ring.tile([P, N], F32, name="back_ps", tag="ring")
+                nc.tensor.transpose(back_ps[:], root_flipped[:, b % R, :], ident[:])
                 rden = held.tile([P, N], F32, name=f"rden{b}")
                 nc.scalar.activation(rden[:], back_ps[:], SQUARE)
                 rden_of[b] = rden
@@ -158,18 +164,24 @@ def tile_slidingwindowattention_s_kernel(tc, x, wq, bq, wv, bv, base, offs, out)
             nc.vector.tensor_tensor(windows[b][:].indirect(offsets[:]), num_of[b][:], rden_of[b][:], MULT)
             nc.sync.dma_start(out_rows[b // R][:, b % R, :], windows[b][:])
 
-        for b in range(PAIR):
+        for b in range(NB):
             score(b)
-        for first in range(PAIR, NB, PAIR):
-            for b in range(first, first + PAIR):
-                score(b)
-            for b in range(first - PAIR, first):
-                weigh(b)
-                add_den(b)
-        for b in range(NB - PAIR, NB):
+        for b in range(PAIR):
             weigh(b)
+            add_num(nc.gpsimd, b)
+        for b in range(R):
             add_den(b)
-        for bank in range(BANKS):
-            invert(bank)
+        for b in range(PAIR, R):
+            weigh(b)
+            add_num(nc.vector if b == R - 1 else nc.gpsimd, b)
+        for b in range(R, NB):
+            weigh(b)
+        invert(0)
+        for b in range(R, NB):
+            add_den(b)
+        invert(1)
+        for b in range(R, NB - 1):
+            add_num_on_tensor(b)
+        add_num(nc.vector, NB - 1)
         for b in range(NB):
             place(b)

@@ -99,10 +99,11 @@ def tile_slidingwindowattention_s_kernel(tc, x, wq, bq, wv, bv, base, offs, out)
 
         def project(name, loads, b, x_rows):
             product = psum_ring.tile([P, x_rows.shape[2]], F32, name=name, tag="ring")
-            for k in range(NB):
+            rows = list(range(NB)) if b // PAIR % 2 == 0 else list(range(R, NB)) + list(range(R))
+            for k in rows:
                 w_rows = loads[b // R, k // R][:].rearrange("p k (m r) -> p k r m", r=R)
                 nc.tensor.matmul(product[:], lhsT=w_rows[:, k % R, b % R, :], rhs=x_rows[:, k, :],
-                                 start=(k == 0), stop=(k == NB - 1))
+                                 start=(k == rows[0]), stop=(k == rows[-1]))
             return product
 
         def score(b):

@@ -9,7 +9,6 @@ MULT = mybir.AluOpType.mult
 EXP = mybir.ActivationFunctionType.Exp
 ABS_RSQRT = mybir.ActivationFunctionType.Abs_reciprocal_sqrt
 SQUARE = mybir.ActivationFunctionType.Square
-COPY = mybir.ActivationFunctionType.Copy
 
 P = 128
 C = 1024
@@ -136,14 +135,6 @@ def tile_slidingwindowattention_s_kernel(tc, x, wq, bq, wv, bv, base, offs, out)
             num_of[b] = held.tile([P, N], F32, name=f"num{b}")
             engine.tensor_tensor(num_of[b][:], four[:], rows[:, 4, :], ADD)
 
-        def add_num_on_tensor(b):
-            num_ps = psum_ring.tile([P, N], F32, name="num_ps", tag="ring")
-            for t in range(T):
-                nc.tensor.matmul(num_ps[:], lhsT=ident[:], rhs=by_query(weighed_of[b])[:, t, :],
-                                 start=(t == 0), stop=(t == T - 1))
-            num_of[b] = held.tile([P, N], F32, name=f"num{b}")
-            nc.scalar.activation(num_of[b][:], num_ps[:], COPY)
-
         def add_den(b):
             if b % R == 0:
                 den_flipped_of[b // R] = psum_flipped.tile([P, R, P], F32, name="den_flipped")
@@ -177,12 +168,10 @@ def tile_slidingwindowattention_s_kernel(tc, x, wq, bq, wv, bv, base, offs, out)
             add_num(nc.vector if b == R - 1 else nc.gpsimd, b)
         for b in range(R, NB):
             weigh(b)
+            add_num(nc.vector, b)
         invert(0)
         for b in range(R, NB):
             add_den(b)
         invert(1)
-        for b in range(R, NB - 1):
-            add_num_on_tensor(b)
-        add_num(nc.vector, NB - 1)
         for b in range(NB):
             place(b)

@@ -20,6 +20,7 @@ NB = C // P
 HALVES = 2
 R = NB // HALVES
 PAIR = 2
+GPSIMD_SUMS = 5
 KEYS = N + 2 * W
 STEP = KEYS + 1
 XREP = 672
@@ -68,9 +69,9 @@ def tile_slidingwindowattention_s_kernel(tc, x, wq, bq, wv, bv, base, offs, out)
 
         load_weights("wq", wq_loads, wq_rows, 0)
         load_bias(0, bq)
-        load_weights("wq", wq_loads, wq_rows, 1)
         load_weights("wv", wv_loads, wv_rows, 0)
         load_bias(NB, bv)
+        load_weights("wq", wq_loads, wq_rows, 1)
         load_weights("wv", wv_loads, wv_rows, 1)
         nc.sync.dma_start(offsets[:], offs)
         for b in range(NB):
@@ -113,10 +114,8 @@ def tile_slidingwindowattention_s_kernel(tc, x, wq, bq, wv, bv, base, offs, out)
             nc.vector.scalar_tensor_tensor(
                 out=scores[:, b % PAIR, :, :], in0=q_ps[:].unsqueeze(1).to_broadcast([P, T, N]),
                 scalar=bias[:, b : b + 1], in1=by_query(xrep[:, b, :]), op0=ADD, op1=MULT)
-            e_pair = e_pairs[b // PAIR]
-            if b % PAIR == PAIR - 1:
-                nc.scalar.activation(e_pair[:].rearrange("p h (t s) -> p h t s", s=STEP)[:, :, :, 0:N], scores[:], EXP)
-            e_of[b] = e_pair[:, b % PAIR, :]
+            e_of[b] = e_pairs[b // PAIR][:, b % PAIR, :]
+            nc.scalar.activation(by_query(e_of[b]), scores[:, b % PAIR, :, :], EXP)
 
         def weigh(b):
             v_ps = project("v_ps", wv_loads, b, xrep[:, :, 0:KEYS])
@@ -143,7 +142,7 @@ def tile_slidingwindowattention_s_kernel(tc, x, wq, bq, wv, bv, base, offs, out)
                                  rhs=ident[:], is_transpose=True, start=(t == 0), stop=(t == T - 1))
 
         def invert(half):
-            root_flipped = scores_of[NB // PAIR - 1][:, half, 0:R, :]
+            root_flipped = scores_of[NB // PAIR - 1][:, PAIR - 1 - half, 0:R, :]
             nc.scalar.activation(root_flipped, den_flipped_of[half][:], ABS_RSQRT)
             for b in range(half * R, (half + 1) * R):
                 back_ps = psum_ring.tile([P, N], F32, name="back_ps", tag="ring")
@@ -156,19 +155,18 @@ def tile_slidingwindowattention_s_kernel(tc, x, wq, bq, wv, bv, base, offs, out)
             nc.vector.tensor_tensor(windows[b][:].indirect(offsets[:]), num_of[b][:], rden_of[b][:], MULT)
             nc.sync.dma_start(out_rows[b // R][:, b % R, :], windows[b][:])
 
-        for b in range(NB):
+        for b in range(R):
             score(b)
-        for b in range(PAIR):
+        for b in range(R):
             weigh(b)
             add_num(nc.gpsimd, b)
+        for b in range(R, NB):
+            score(b)
         for b in range(R):
             add_den(b)
-        for b in range(PAIR, R):
-            weigh(b)
-            add_num(nc.vector if b == R - 1 else nc.gpsimd, b)
         for b in range(R, NB):
             weigh(b)
-            add_num(nc.vector, b)
+            add_num(nc.gpsimd if b < GPSIMD_SUMS else nc.vector, b)
         invert(0)
         for b in range(R, NB):
             add_den(b)

@@ -9,6 +9,7 @@ MULT = mybir.AluOpType.mult
 EXP = mybir.ActivationFunctionType.Exp
 ABS_RSQRT = mybir.ActivationFunctionType.Abs_reciprocal_sqrt
 SQUARE = mybir.ActivationFunctionType.Square
+COPY = mybir.ActivationFunctionType.Copy
 
 P = 128
 C = 1024
@@ -19,8 +20,8 @@ T = 2 * W + 1
 NB = C // P
 HALVES = 2
 R = NB // HALVES
+TENSOR_SUMS = (R, NB - 2)
 PAIR = 2
-GPSIMD_SUMS = 5
 KEYS = N + 2 * W
 STEP = KEYS + 1
 XREP = 672
@@ -134,6 +135,14 @@ def tile_slidingwindowattention_s_kernel(tc, x, wq, bq, wv, bv, base, offs, out)
             num_of[b] = held.tile([P, N], F32, name=f"num{b}")
             engine.tensor_tensor(num_of[b][:], four[:], rows[:, 4, :], ADD)
 
+        def add_num_on_tensor(b):
+            num_ps = psum_ring.tile([P, N], F32, name="num_ps", tag="ring")
+            for t in range(T):
+                nc.tensor.matmul(num_ps[:], lhsT=ident[:], rhs=by_query(weighed_of[b])[:, t, :],
+                                 start=(t == 0), stop=(t == T - 1))
+            num_of[b] = held.tile([P, N], F32, name=f"num{b}")
+            nc.scalar.activation(num_of[b][:], num_ps[:], COPY)
+
         def add_den(b):
             if b % R == 0:
                 den_flipped_of[b // R] = psum_flipped.tile([P, R, P], F32, name="den_flipped")
@@ -141,12 +150,14 @@ def tile_slidingwindowattention_s_kernel(tc, x, wq, bq, wv, bv, base, offs, out)
                 nc.tensor.matmul(den_flipped_of[b // R][:, b % R, :], lhsT=by_query(e_of[b])[:, t, :],
                                  rhs=ident[:], is_transpose=True, start=(t == 0), stop=(t == T - 1))
 
-        def invert(half):
-            root_flipped = scores_of[NB // PAIR - 1][:, PAIR - 1 - half, 0:R, :]
-            nc.scalar.activation(root_flipped, den_flipped_of[half][:], ABS_RSQRT)
-            for b in range(half * R, (half + 1) * R):
+        def invert(pair):
+            first = pair * PAIR
+            half, rows = first // R, slice(first % R, first % R + PAIR)
+            root_flipped = scores_of[NB // PAIR - 1][:, PAIR - 1 - half, rows, :]
+            nc.scalar.activation(root_flipped, den_flipped_of[half][:, rows, :], ABS_RSQRT)
+            for b in range(first, first + PAIR):
                 back_ps = psum_ring.tile([P, N], F32, name="back_ps", tag="ring")
-                nc.tensor.transpose(back_ps[:], root_flipped[:, b % R, :], ident[:])
+                nc.tensor.transpose(back_ps[:], root_flipped[:, b - first, :], ident[:])
                 rden = held.tile([P, N], F32, name=f"rden{b}")
                 nc.scalar.activation(rden[:], back_ps[:], SQUARE)
                 rden_of[b] = rden
@@ -166,10 +177,15 @@ def tile_slidingwindowattention_s_kernel(tc, x, wq, bq, wv, bv, base, offs, out)
             add_den(b)
         for b in range(R, NB):
             weigh(b)
-            add_num(nc.gpsimd if b < GPSIMD_SUMS else nc.vector, b)
-        invert(0)
+            if b not in TENSOR_SUMS:
+                add_num(nc.vector if b == NB - 1 else nc.gpsimd, b)
+        add_num_on_tensor(TENSOR_SUMS[0])
+        for pair in range(R // PAIR):
+            invert(pair)
         for b in range(R, NB):
             add_den(b)
-        invert(1)
+        for pair in range(R // PAIR, NB // PAIR):
+            invert(pair)
+        add_num_on_tensor(TENSOR_SUMS[1])
         for b in range(NB):
             place(b)

import concourse.mybir as mybir
from concourse.masks import make_identity

F32 = mybir.dt.float32
BF16 = mybir.dt.bfloat16
U16 = mybir.dt.uint16
ADD = mybir.AluOpType.add
MULT = mybir.AluOpType.mult
EXP = mybir.ActivationFunctionType.Exp
ABS_RSQRT = mybir.ActivationFunctionType.Abs_reciprocal_sqrt
SQUARE = mybir.ActivationFunctionType.Square
COPY = mybir.ActivationFunctionType.Copy

P = 128
C = 1024
N = 128
S = 256
W = 2
T = 2 * W + 1
NB = C // P
HALVES = 2
R = NB // HALVES
TENSOR_SUMS = (R, NB - 2)
PAIR = 2
KEYS = N + 2 * W
STEP = KEYS + 1
XREP = 672

FLOPS = 2 * 2 * C * C * N


def by_query(rows):
    return rows[:, 0 : T * STEP].rearrange("p (t s) -> p t s", s=STEP)[:, :, 0:N]


def by_key(rows):
    return rows[:, 0 : T * KEYS].rearrange("p (t k) -> p t k", k=KEYS)


def tile_slidingwindowattention_s_kernel(tc, x, wq, bq, wv, bv, base, offs, out):
    nc = tc.nc
    half_cols = C // HALVES
    wq_rows = wq.rearrange("(h p r) c -> h p r c", h=HALVES, p=P)
    wv_rows = wv.rearrange("(h p r) c -> h p r c", h=HALVES, p=P)
    base_rows = base.rearrange("(h p r) s -> h p r s", h=HALVES, p=P)
    out_rows = out.rearrange("(h p r) s -> h p r s", h=HALVES, p=P)

    with (
        tc.tile_pool(name="held", bufs=1) as held,
        tc.tile_pool(name="work", bufs=4) as work,
        tc.psum_pool(name="psum_ring", bufs=6) as psum_ring,
        tc.psum_pool(name="psum_flipped", bufs=HALVES) as psum_flipped,
    ):
        xt = held.tile([P, NB, N], BF16, name="xt")
        nc.sync.dma_start(xt[:].rearrange("p (h r) j -> p h (r j)", h=HALVES),
                          x.rearrange("(h p r) j -> p h (r j)", h=HALVES, p=P))
        bias = held.tile([P, 2 * NB], F32, name="bias")
        offsets = held.tile([P, N // 16], U16, name="offsets")
        wq_loads, wv_loads, windows = {}, {}, []

        def load_weights(name, loads, rows, half):
            for k_half in range(HALVES):
                loads[half, k_half] = held.tile([P, R, half_cols], BF16, name=f"{name}{half}{k_half}")
                nc.sync.dma_start(loads[half, k_half][:],
                                  rows[k_half][:, :, half * half_cols : (half + 1) * half_cols])

        def load_bias(column, bias_dram):
            nc.sync.dma_start(bias[:, column : column + NB].rearrange("p (h r) -> p h r", h=HALVES),
                              bias_dram.rearrange("(h p r) o -> p h (r o)", h=HALVES, p=P))

        load_weights("wq", wq_loads, wq_rows, 0)
        load_bias(0, bq)
        load_weights("wv", wv_loads, wv_rows, 0)
        load_bias(NB, bv)
        load_weights("wq", wq_loads, wq_rows, 1)
        load_weights("wv", wv_loads, wv_rows, 1)
        nc.sync.dma_start(offsets[:], offs)
        for b in range(NB):
            window = held.tile([P, S], F32, name=f"window{b}")
            nc.sync.dma_start(window[:], base_rows[b // R][:, b % R, :])
            windows.append(window)

        xrep = held.tile([P, NB, XREP], BF16, name="xrep")
        nc.vector.tensor_copy(xrep[:, :, W : W + N], xt[:])
        nc.vector.tensor_copy(xrep[:, :, 0:W], xt[:, :, N - W : N])
        nc.vector.tensor_copy(xrep[:, :, W + N : KEYS], xt[:, :, 0:W])
        for t in range(1, T):
            nc.vector.tensor_copy(xrep[:, :, t * KEYS : (t + 1) * KEYS], xrep[:, :, 0:KEYS])

        ident = held.tile([P, P], F32, name="ident")
        make_identity(nc, ident[:])

        e_pairs = []
        for i in range(NB // PAIR):
            e_pair = held.tile([P, PAIR, T * STEP], F32, name=f"e{i}")
            nc.vector.memset(e_pair[:].rearrange("p h (t s) -> p h t s", s=STEP)[:, :, :, N:STEP], 0.0)
            e_pairs.append(e_pair)

        scores_of, e_of, weighed_of, num_of, den_flipped_of, rden_of = {}, {}, {}, {}, {}, {}

        def project(name, loads, b, x_rows):
            product = psum_ring.tile([P, x_rows.shape[2]], F32, name=name, tag="ring")
            rows = list(range(NB)) if b // PAIR % 2 == 0 else list(range(R, NB)) + list(range(R))
            for k in rows:
                w_rows = loads[b // R, k // R][:].rearrange("p k (m r) -> p k r m", r=R)
                nc.tensor.matmul(product[:], lhsT=w_rows[:, k % R, b % R, :], rhs=x_rows[:, k, :],
                                 start=(k == rows[0]), stop=(k == rows[-1]))
            return product

        def score(b):
            q_ps = project("q_ps", wq_loads, b, xt[:])
            if b % PAIR == 0:
                scores_of[b // PAIR] = work.tile([P, PAIR, T, N], F32, name="scores")
            scores = scores_of[b // PAIR]
            nc.vector.scalar_tensor_tensor(
                out=scores[:, b % PAIR, :, :], in0=q_ps[:].unsqueeze(1).to_broadcast([P, T, N]),
                scalar=bias[:, b : b + 1], in1=by_query(xrep[:, b, :]), op0=ADD, op1=MULT)
            e_of[b] = e_pairs[b // PAIR][:, b % PAIR, :]
            nc.scalar.activation(by_query(e_of[b]), scores[:, b % PAIR, :, :], EXP)

        def weigh(b):
            v_ps = project("v_ps", wv_loads, b, xrep[:, :, 0:KEYS])
            weighed = held.tile([P, T * STEP], F32, name=f"weighed{b}")
            nc.vector.scalar_tensor_tensor(
                out=by_key(weighed), in0=v_ps[:].unsqueeze(1).to_broadcast([P, T, KEYS]),
                scalar=bias[:, NB + b : NB + b + 1], in1=by_key(e_of[b]), op0=ADD, op1=MULT)
            weighed_of[b] = weighed

        def add_num(engine, b):
            rows = by_query(weighed_of[b])
            two = work.tile([P, 2, N], F32, name="two")
            engine.tensor_tensor(two[:], rows[:, 0:2, :], rows[:, 2:4, :], ADD)
            four = work.tile([P, N], F32, name="four")
            engine.tensor_tensor(four[:], two[:, 0, :], two[:, 1, :], ADD)
            num_of[b] = held.tile([P, N], F32, name=f"num{b}")
            engine.tensor_tensor(num_of[b][:], four[:], rows[:, 4, :], ADD)

        def add_num_on_tensor(b):
            num_ps = psum_ring.tile([P, N], F32, name="num_ps", tag="ring")
            for t in range(T):
                nc.tensor.matmul(num_ps[:], lhsT=ident[:], rhs=by_query(weighed_of[b])[:, t, :],
                                 start=(t == 0), stop=(t == T - 1))
            num_of[b] = held.tile([P, N], F32, name=f"num{b}")
            nc.scalar.activation(num_of[b][:], num_ps[:], COPY)

        def add_den(b):
            if b % R == 0:
                den_flipped_of[b // R] = psum_flipped.tile([P, R, P], F32, name="den_flipped")
            for t in range(T):
                nc.tensor.matmul(den_flipped_of[b // R][:, b % R, :], lhsT=by_query(e_of[b])[:, t, :],
                                 rhs=ident[:], is_transpose=True, start=(t == 0), stop=(t == T - 1))

        def invert(pair):
            first = pair * PAIR
            half, rows = first // R, slice(first % R, first % R + PAIR)
            root_flipped = scores_of[NB // PAIR - 1][:, PAIR - 1 - half, rows, :]
            nc.scalar.activation(root_flipped, den_flipped_of[half][:, rows, :], ABS_RSQRT)
            for b in range(first, first + PAIR):
                back_ps = psum_ring.tile([P, N], F32, name="back_ps", tag="ring")
                nc.tensor.transpose(back_ps[:], root_flipped[:, b - first, :], ident[:])
                rden = held.tile([P, N], F32, name=f"rden{b}")
                nc.scalar.activation(rden[:], back_ps[:], SQUARE)
                rden_of[b] = rden

        def place(b):
            nc.vector.tensor_tensor(windows[b][:].indirect(offsets[:]), num_of[b][:], rden_of[b][:], MULT)
            nc.sync.dma_start(out_rows[b // R][:, b % R, :], windows[b][:])

        for b in range(R):
            score(b)
        for b in range(R):
            weigh(b)
            add_num(nc.gpsimd, b)
        for b in range(R, NB):
            score(b)
        for b in range(R):
            add_den(b)
        for b in range(R, NB):
            weigh(b)
            if b not in TENSOR_SUMS:
                add_num(nc.vector if b == NB - 1 else nc.gpsimd, b)
        add_num_on_tensor(TENSOR_SUMS[0])
        for pair in range(R // PAIR):
            invert(pair)
        for b in range(R, NB):
            add_den(b)
        for pair in range(R // PAIR, NB // PAIR):
            invert(pair)
        add_num_on_tensor(TENSOR_SUMS[1])
        for b in range(NB):
            place(b)
